import numpy as np
import ml_dtypes


def mxq(x, axis, fmt="e4m3"):
    dtype, down = {"e4m3": (ml_dtypes.float8_e4m3fn, 7), "e5m2": (ml_dtypes.float8_e5m2, 14)}[fmt]
    v = np.moveaxis(np.asarray(x, np.float32).astype(ml_dtypes.bfloat16).astype(np.float64), axis, -1)
    blocks = v.reshape(v.shape[:-1] + (-1, 32))
    amax = np.abs(blocks).max(-1, keepdims=True)
    byte = np.maximum(np.where(amax > 0, np.frexp(amax)[1] - 1 + 127, 0) - down, 1)
    scale = np.exp2(byte - 127.0)
    codes = (blocks / scale).astype(np.float32).astype(dtype).astype(np.float64)
    return np.moveaxis((codes * scale).reshape(v.shape), -1, axis)


WIDE = False


def mx_kscale(k):
    if not WIDE:
        return np.ones(k)
    levels = np.array([10, -10, 5, -5, 0])
    if k % 512:
        return np.exp2(np.random.permutation(np.resize(levels, k // 32))).repeat(32)
    a = np.empty((k // 512, 16))
    for p in range(k // 512):
        a[p, :8] = np.random.permutation(np.resize(levels, 8))
        for g in range(8):
            far = levels[np.abs(levels - a[p, g]) >= 10]
            a[p, g + 8] = far[np.random.randint(len(far))]
    return np.exp2(a.ravel()).repeat(32)


BF16 = ml_dtypes.bfloat16


def bf(x):
    return np.asarray(x, np.float32).astype(BF16)


def f64(x):
    return np.asarray(x).astype(np.float64)


B, S, DM, H, DH, QB = 4, 2048, 256, 4, 256, 512
DI = H * DH
EPS_GN = 1e-5


def setup_inputs():
    s = mx_kscale(DI)
    h = np.random.standard_normal((B, S, H, DH)) * 0.15 + np.random.standard_normal((B, 1, H, 1)) * 0.15
    return {"h_attn": bf(h.reshape(B, S, DI)),
            "gn_w": bf((1.0 + 0.1 * np.random.standard_normal(DI)) * s),
            "gn_b": bf(0.1 * np.random.standard_normal(DI) * s),
            "W_out": bf(np.random.standard_normal((DM, DI)) / np.sqrt(DI) / s[None, :]),
            "x": bf(np.random.standard_normal((B, S, DM))),
            "skip_scale": bf(0.7 + 0.1 * np.random.standard_normal(1))}


def reference(h_attn, gn_w, gn_b, W_out, x, skip_scale):
    hg = f64(h_attn).reshape(B, S, H, DH)
    mu = hg.mean(axis=(1, 3), keepdims=True)
    var = hg.var(axis=(1, 3), keepdims=True)
    hg = (hg - mu) / np.sqrt(var + EPS_GN)
    h = hg.reshape(B, S, DI) * f64(gn_w) + f64(gn_b)
    return (mxq(h, 2, "e4m3") @ mxq(f64(W_out), 1, "e4m3").T) + f64(skip_scale) * f64(x)

@@ -1,0 +1,296 @@
+from contextlib import ExitStack
+
+import concourse.mybir as mybir
+from concourse.masks import make_identity
+
+FP8X4 = mybir.dt.float8_e4m3fn_x4
+BF16 = mybir.dt.bfloat16
+F32 = mybir.dt.float32
+U32 = mybir.dt.uint32
+U8 = mybir.dt.uint8
+ALU = mybir.AluOpType
+ACT = mybir.ActivationFunctionType
+AXIS = mybir.AxisListType
+
+P = 128
+PACK = 4
+K_PASS = P * PACK
+
+BATCH, SEQ, CHANNELS, D_MODEL = 4, 2048, 1024, 256
+GROUP = 256
+EPS = 1e-5
+
+PASSES = CHANNELS // K_PASS
+GROUPS_PER_PASS = K_PASS // GROUP
+TILES_PER_GROUP = GROUP // P
+ROWS = SEQ // P
+HALVES = 2
+HALF_ROWS = ROWS // HALVES
+HALF_TOKENS = HALF_ROWS * P
+ROWS_PER_BANK = 2
+
+RESIDENT = 3
+UNITS_PER_BATCH = PASSES * HALVES
+
+FLOPS = 2 * BATCH * SEQ * CHANNELS * D_MODEL
+
+
+def tile_mlstmblock_pb_t_kernel(tc, h_attn, gn_w, gn_b, W_out, x, skip_scale, out):
+    nc = tc.nc
+    h_view = h_attn.rearrange("b (p r) c -> b p r c", r=ROWS)
+    x_view = x.rearrange("b (p r) d -> b p r d", r=ROWS)
+    out_view = out.rearrange("b (p r) d -> b p r d", r=ROWS)
+
+    with ExitStack() as ctx:
+        consts = ctx.enter_context(tc.tile_pool(name="consts", bufs=1))
+        h_pool = ctx.enter_context(tc.tile_pool(name="h_pool", bufs=RESIDENT * UNITS_PER_BATCH))
+        x_pool = ctx.enter_context(tc.tile_pool(name="x_pool", bufs=3))
+        work = ctx.enter_context(tc.tile_pool(name="work", bufs=2))
+        codes_pool = ctx.enter_context(tc.tile_pool(name="codes_pool", bufs=1))
+        stat_pool = ctx.enter_context(tc.tile_pool(name="stat_pool", bufs=3))
+        tp_psum = ctx.enter_context(tc.psum_pool(name="tp_psum", bufs=PACK))
+        mm_psum = ctx.enter_context(tc.psum_pool(name="mm_psum", bufs=2))
+        stat_psum = ctx.enter_context(tc.psum_pool(name="stat_psum", bufs=PASSES))
+
+        h_tiles = {}
+        x_tiles = {}
+
+        def load_h(b, k, half):
+            h_tile = h_pool.tile([P, HALF_ROWS, K_PASS], BF16, name="h_tile")
+            nc.sync.dma_start(
+                out=h_tile[:],
+                in_=h_view[b, :, half * HALF_ROWS : (half + 1) * HALF_ROWS, k * K_PASS : (k + 1) * K_PASS],
+            )
+            h_tiles[(b, k, half)] = h_tile
+
+        def load_x(b, half):
+            x_tile = x_pool.tile([P, HALF_ROWS, D_MODEL], BF16, name="x_tile")
+            nc.sync.dma_start(out=x_tile[:], in_=x_view[b, :, half * HALF_ROWS : (half + 1) * HALF_ROWS, :])
+            x_tiles[(b, half)] = x_tile
+
+        ident = consts.tile([P, P], BF16, name="ident")
+        make_identity(nc, ident[:])
+        ones_col = consts.tile([P, 2], BF16, name="ones_col")
+        nc.vector.memset(ones_col[:], -1.0)
+        mean_mat = consts.tile([P, GROUPS_PER_PASS, P], F32, name="mean_mat")
+        nc.vector.memset(mean_mat[:], 0.0)
+        for g in range(GROUPS_PER_PASS):
+            g0 = g * GROUP // PACK
+            nc.vector.memset(mean_mat[:, g, g0 : g0 + GROUP // PACK], 1.0 / (SEQ * GROUP))
+        warm = consts.tile([P, 1], F32, name="warm")
+        nc.vector.memset(warm[:], 1.0)
+        nc.scalar.activation(out=warm[:], in_=warm[:], func=ACT.Sqrt)
+
+        gn_rows = consts.tile([P, K_PASS], BF16, name="gn_rows")
+        nc.vector.memset(gn_rows[:], 0.0)
+        nc.scalar.dma_start(out=gn_rows[0:PASSES, :], in_=gn_w.rearrange("(k c) -> k c", k=PASSES))
+        nc.scalar.dma_start(out=gn_rows[PASSES : 2 * PASSES, :], in_=gn_b.rearrange("(k c) -> k c", k=PASSES))
+        skip_bf = consts.tile([P, 1], BF16, name="skip_bf")
+        nc.scalar.dma_start(out=skip_bf[:], in_=skip_scale.partition_broadcast(P))
+
+        load_h(0, 0, 0)
+        load_h(0, 0, 1)
+        w_raw = consts.tile([P, D_MODEL // P, CHANNELS], BF16, name="w_raw")
+        nc.sync.dma_start(out=w_raw[:], in_=W_out.rearrange("(m p) c -> p m c", p=P))
+        load_h(0, 1, 0)
+        load_h(0, 1, 1)
+        load_x(0, 0)
+        load_x(0, 1)
+        for b in range(1, RESIDENT):
+            for k in range(PASSES):
+                for half in range(HALVES):
+                    load_h(b, k, half)
+
+        gn_ps = tp_psum.tile([P, HALF_TOKENS], BF16, name="tp")
+        for t in range(PACK):
+            nc.tensor.transpose(gn_ps[:, t * P : (t + 1) * P], gn_rows[:, t :: PACK], ident[:])
+        gn_cols = consts.tile([P, 2 * PASSES, PACK], F32, name="gn_cols")
+        nc.vector.tensor_copy(
+            out=gn_cols[:], in_=gn_ps[:, 0 : PACK * P].rearrange("p (t m) -> p m t", t=PACK)[:, 0 : 2 * PASSES, :]
+        )
+        skip_f = consts.tile([P, 1], F32, name="skip_f")
+        nc.vector.tensor_copy(out=skip_f[:], in_=skip_bf[:])
+
+        parts = {}
+        stat_banks = {}
+        scale_bias = {}
+
+        def start_stats(b, k):
+            parts[(b, k)] = stat_pool.tile([P, 2, 8], F32, name="parts")
+            stat_banks[(b, k)] = stat_psum.tile([P, 16], F32, name="stat_bank")
+
+        def square_sums(b, k, half):
+            for g in range(GROUPS_PER_PASS):
+                squares = work.tile([P, HALF_ROWS, GROUP], BF16, name="squares")
+                nc.scalar.activation(
+                    out=squares[:],
+                    in_=h_tiles[(b, k, half)][:, :, g * GROUP : (g + 1) * GROUP],
+                    func=ACT.Square,
+                    accum_out=parts[(b, k)][:, 1, g * HALVES + half : g * HALVES + half + 1],
+                )
+
+        def channel_sums(b, k, half):
+            for t in range(PACK):
+                col = t * HALVES + half
+                for r in range(HALF_ROWS):
+                    nc.tensor.matmul(
+                        out=stat_banks[(b, k)][:, col : col + 1],
+                        lhsT=h_tiles[(b, k, half)][:, r, t * P : (t + 1) * P],
+                        rhs=ones_col[:, 0:1],
+                        start=(r == 0),
+                        stop=(r == HALF_ROWS - 1),
+                    )
+
+        def finish_stats(b, k):
+            bank = stat_banks[(b, k)]
+            n_sum = PACK * HALVES
+            n_part = GROUPS_PER_PASS * HALVES
+            nc.vector.tensor_reduce(
+                out=parts[(b, k)][:, 0, 0:n_part].rearrange("p (g s) -> p g s", g=GROUPS_PER_PASS),
+                in_=bank[:, 0:n_sum].rearrange("p (g j s) -> p g s j", g=GROUPS_PER_PASS, j=TILES_PER_GROUP),
+                axis=AXIS.X,
+                op=ALU.add,
+            )
+            sums = bank[:, n_sum : n_sum + 2 * HALVES].rearrange("p (a s) -> p a s", a=2)
+            for g in range(GROUPS_PER_PASS):
+                nc.tensor.matmul(
+                    out=sums,
+                    lhsT=mean_mat[:, g, :],
+                    rhs=parts[(b, k)][:, :, g * HALVES : (g + 1) * HALVES],
+                    start=(g == 0),
+                    stop=(g == GROUPS_PER_PASS - 1),
+                )
+            both = stat_pool.tile([P, 2], F32, name="both")
+            nc.vector.tensor_reduce(out=both[:], in_=sums, axis=AXIS.X, op=ALU.add)
+            neg_mean = both[:, 0:1]
+            ex2 = both[:, 1:2]
+            mean_sq = stat_pool.tile([P, 1], F32, name="mean_sq")
+            nc.scalar.activation(out=mean_sq[:], in_=neg_mean, func=ACT.Square)
+            var_eps = stat_pool.tile([P, 1], F32, name="var_eps")
+            nc.vector.scalar_tensor_tensor(
+                out=var_eps[:], in0=ex2, scalar=EPS, in1=mean_sq[:], op0=ALU.add, op1=ALU.subtract
+            )
+            std = stat_pool.tile([P, 1], F32, name="std")
+            nc.scalar.activation(out=std[:], in_=var_eps[:], func=ACT.Sqrt)
+            rstd = stat_pool.tile([P, 1], F32, name="rstd")
+            nc.vector.reciprocal(out=rstd[:], in_=std[:])
+            scale = stat_pool.tile([P, PACK], F32, name="scale")
+            nc.vector.tensor_scalar(out=scale[:], in0=gn_cols[:, k, :], scalar1=rstd[:, 0:1], scalar2=None, op0=ALU.mult)
+            bias = stat_pool.tile([P, PACK], F32, name="bias")
+            nc.vector.scalar_tensor_tensor(
+                out=bias[:], in0=scale[:], scalar=neg_mean, in1=gn_cols[:, PASSES + k, :], op0=ALU.mult, op1=ALU.add
+            )
+            scale_bias[(b, k)] = (scale, bias)
+
+        w_grouped = consts.tile([P, PASSES, D_MODEL, PACK], BF16, name="w_grouped", align_bytes=64)
+        w_codes = consts.tile([P, PASSES * D_MODEL], U32, name="w_codes", align_bytes=64)
+        w_scales = consts.tile([P, PASSES * D_MODEL], U8, name="w_scales", align_bytes=64)
+
+        def prepare_w():
+            for k in range(PASSES):
+                w_ps = tp_psum.tile([P, PACK * D_MODEL], BF16, name="tp")
+                for t in range(PACK):
+                    for m in range(D_MODEL // P):
+                        nc.tensor.transpose(
+                            w_ps[:, t * D_MODEL + m * P : t * D_MODEL + (m + 1) * P], w_raw[:, m, k * K_PASS + t : (k + 1) * K_PASS : PACK], ident[:]
+                        )
+                nc.vector.tensor_copy(out=w_grouped[:, k], in_=w_ps[:].rearrange("p (t n) -> p n t", t=PACK))
+            nc.vector.quantize_mx(
+                out=w_codes[:].bitcast(FP8X4),
+                scales=w_scales[:],
+                in_=w_grouped[:].rearrange("p k n t -> p (k n t)"),
+            )
+
+        h_codes = {}
+
+        def normalise(b, k, half):
+            scale, bias = scale_bias[(b, k)]
+            planes = work.tile([P, PACK, HALF_TOKENS], BF16, name="planes")
+            on_scalar = 1 + half
+            for t in range(PACK):
+                tp = tp_psum.tile([P, HALF_TOKENS], BF16, name="tp")
+                for r in range(HALF_ROWS):
+                    nc.tensor.transpose(tp[:, r * P : (r + 1) * P], h_tiles[(b, k, half)][:, r, t::PACK], ident[:])
+                if t >= PACK - on_scalar:
+                    nc.scalar.activation(
+                        out=planes[:, t, :], in_=tp[:], func=ACT.Identity, scale=scale[:, t : t + 1], bias=bias[:, t : t + 1]
+                    )
+                else:
+                    nc.vector.tensor_scalar(
+                        out=planes[:, t, :],
+                        in0=tp[:],
+                        scalar1=scale[:, t : t + 1],
+                        scalar2=bias[:, t : t + 1],
+                        op0=ALU.mult,
+                        op1=ALU.add,
+                    )
+            return planes
+
+        def quantise(b, k, half, planes):
+            grouped = work.tile([P, HALF_TOKENS, PACK], BF16, name="grouped", align_bytes=64)
+            nc.vector.tensor_copy(
+                out=grouped[:].rearrange("p (c i) t -> p c t i", i=4),
+                in_=planes[:].rearrange("p t (c i) -> p c t i", i=4),
+            )
+            codes = codes_pool.tile([P, HALF_TOKENS], U32, name="codes%d%d" % (k, half), align_bytes=64)
+            scales = codes_pool.tile([P, HALF_TOKENS], U8, name="scales%d%d" % (k, half), align_bytes=64)
+            nc.vector.quantize_mx(
+                out=codes[:].bitcast(FP8X4), scales=scales[:], in_=grouped[:].rearrange("p r t -> p (r t)")
+            )
+            h_codes[(k, half)] = (codes, scales)
+
+        def project(b, half):
+            result = work.tile([P, HALF_ROWS, D_MODEL], F32, name="result")
+            for pair in range(HALF_ROWS // ROWS_PER_BANK):
+                acc = mm_psum.tile([P, ROWS_PER_BANK, D_MODEL], F32, name="acc")
+                for s in range(ROWS_PER_BANK):
+                    r = ROWS_PER_BANK * pair + s
+                    for k in range(PASSES):
+                        codes, scales = h_codes[(k, half)]
+                        nc.tensor.matmul_mx(
+                            out=acc[:, s, :],
+                            lhsT=codes[:, r * P : (r + 1) * P].bitcast(FP8X4),
+                            lhsT_scale=scales[:, r * P : (r + 1) * P],
+                            rhs=w_codes[:, k * D_MODEL : (k + 1) * D_MODEL].bitcast(FP8X4),
+                            rhs_scale=w_scales[:, k * D_MODEL : (k + 1) * D_MODEL],
+                            start=(k == 0),
+                            stop=(k == PASSES - 1),
+                        )
+                rows = slice(ROWS_PER_BANK * pair, ROWS_PER_BANK * (pair + 1))
+                nc.vector.scalar_tensor_tensor(
+                    out=result[:, rows, :].rearrange("p s d -> p (s d)"),
+                    in0=x_tiles[(b, half)][:, rows, :].rearrange("p s d -> p (s d)"),
+                    scalar=skip_f[:, 0:1],
+                    in1=acc[:].rearrange("p s d -> p (s d)"),
+                    op0=ALU.mult,
+                    op1=ALU.add,
+                )
+            nc.sync.dma_start(out=out_view[b, :, half * HALF_ROWS : (half + 1) * HALF_ROWS, :], in_=result[:])
+
+        for k in range(PASSES):
+            start_stats(0, k)
+            for half in range(HALVES):
+                square_sums(0, k, half)
+                channel_sums(0, k, half)
+            finish_stats(0, k)
+            if k == 0:
+                prepare_w()
+
+        for b in range(BATCH):
+            for k in range(PASSES):
+                for half in range(HALVES):
+                    planes = normalise(b, k, half)
+                    if b + 1 < BATCH:
+                        if half == 0:
+                            start_stats(b + 1, k)
+                        square_sums(b + 1, k, half)
+                        channel_sums(b + 1, k, half)
+                    quantise(b, k, half, planes)
+                    if b + 1 < BATCH and half == HALVES - 1:
+                        finish_stats(b + 1, k)
+                    if k == PASSES - 1:
+                        project(b, half)
+                    if b + RESIDENT < BATCH:
+                        load_h(b + RESIDENT, k, half)
+                    if b + 1 < BATCH and k == 0:
+                        load_x(b + 1, half)

@@ -22,14 +22,15 @@ EPS = 1e-5
 
 PASSES = CHANNELS // K_PASS
 GROUPS_PER_PASS = K_PASS // GROUP
-TILES_PER_GROUP = GROUP // P
+GROUP_PARTS = GROUP // PACK
 ROWS = SEQ // P
 HALVES = 2
 HALF_ROWS = ROWS // HALVES
 HALF_TOKENS = HALF_ROWS * P
 ROWS_PER_BANK = 2
-
-RESIDENT = 3
+PAIRS = HALF_ROWS // ROWS_PER_BANK
+CHUNK_ROWS = 4
+CHUNKS = ROWS // CHUNK_ROWS
 UNITS_PER_BATCH = PASSES * HALVES
 
 FLOPS = 2 * BATCH * SEQ * CHANNELS * D_MODEL
@@ -43,24 +44,29 @@ def tile_mlstmblock_pb_t_kernel(tc, h_attn, gn_w, gn_b, W_out, x, skip_scale, ou
 
     with ExitStack() as ctx:
         consts = ctx.enter_context(tc.tile_pool(name="consts", bufs=1))
-        h_pool = ctx.enter_context(tc.tile_pool(name="h_pool", bufs=RESIDENT * UNITS_PER_BATCH))
-        x_pool = ctx.enter_context(tc.tile_pool(name="x_pool", bufs=3))
+        h_pool = ctx.enter_context(tc.tile_pool(name="h_pool", bufs=BATCH * UNITS_PER_BATCH))
+        x_pool = ctx.enter_context(tc.tile_pool(name="x_pool", bufs=4))
         work = ctx.enter_context(tc.tile_pool(name="work", bufs=2))
         codes_pool = ctx.enter_context(tc.tile_pool(name="codes_pool", bufs=1))
+        junk_pool = ctx.enter_context(tc.tile_pool(name="junk_pool", bufs=1))
         stat_pool = ctx.enter_context(tc.tile_pool(name="stat_pool", bufs=3))
-        tp_psum = ctx.enter_context(tc.psum_pool(name="tp_psum", bufs=PACK))
+        tp_psum = ctx.enter_context(tc.psum_pool(name="tp_psum", bufs=4))
         mm_psum = ctx.enter_context(tc.psum_pool(name="mm_psum", bufs=2))
-        stat_psum = ctx.enter_context(tc.psum_pool(name="stat_psum", bufs=PASSES))
+        stat_psum = ctx.enter_context(tc.psum_pool(name="stat_psum", bufs=2))
+        ctx.enter_context(tc.manual_schedule())
 
         h_tiles = {}
         x_tiles = {}
 
-        def load_h(b, k, half):
+        def load_h(b, k, half, pieces=1):
             h_tile = h_pool.tile([P, HALF_ROWS, K_PASS], BF16, name="h_tile")
-            nc.sync.dma_start(
-                out=h_tile[:],
-                in_=h_view[b, :, half * HALF_ROWS : (half + 1) * HALF_ROWS, k * K_PASS : (k + 1) * K_PASS],
-            )
+            n = HALF_ROWS // pieces
+            for i in range(pieces):
+                r0 = half * HALF_ROWS + i * n
+                nc.sync.dma_start(
+                    out=h_tile[:, i * n : (i + 1) * n, :],
+                    in_=h_view[b, :, r0 : r0 + n, k * K_PASS : (k + 1) * K_PASS],
+                )
             h_tiles[(b, k, half)] = h_tile
 
         def load_x(b, half):
@@ -68,117 +74,165 @@ def tile_mlstmblock_pb_t_kernel(tc, h_attn, gn_w, gn_b, W_out, x, skip_scale, ou
             nc.sync.dma_start(out=x_tile[:], in_=x_view[b, :, half * HALF_ROWS : (half + 1) * HALF_ROWS, :])
             x_tiles[(b, half)] = x_tile
 
-        ident = consts.tile([P, P], BF16, name="ident")
-        make_identity(nc, ident[:])
-        ones_col = consts.tile([P, 2], BF16, name="ones_col")
-        nc.vector.memset(ones_col[:], -1.0)
-        mean_mat = consts.tile([P, GROUPS_PER_PASS, P], F32, name="mean_mat")
-        nc.vector.memset(mean_mat[:], 0.0)
-        for g in range(GROUPS_PER_PASS):
-            g0 = g * GROUP // PACK
-            nc.vector.memset(mean_mat[:, g, g0 : g0 + GROUP // PACK], 1.0 / (SEQ * GROUP))
-        warm = consts.tile([P, 1], F32, name="warm")
-        nc.vector.memset(warm[:], 1.0)
-        nc.scalar.activation(out=warm[:], in_=warm[:], func=ACT.Sqrt)
-
-        gn_rows = consts.tile([P, K_PASS], BF16, name="gn_rows")
-        nc.vector.memset(gn_rows[:], 0.0)
-        nc.scalar.dma_start(out=gn_rows[0:PASSES, :], in_=gn_w.rearrange("(k c) -> k c", k=PASSES))
-        nc.scalar.dma_start(out=gn_rows[PASSES : 2 * PASSES, :], in_=gn_b.rearrange("(k c) -> k c", k=PASSES))
+        gnw = consts.tile([P, PASSES, PACK], BF16, name="gnw")
+        gnb = consts.tile([P, PASSES, PACK], BF16, name="gnb")
+        nc.scalar.dma_start(out=gnw[:], in_=gn_w.rearrange("(k p t) -> p k t", p=P, t=PACK))
+        nc.scalar.dma_start(out=gnb[:], in_=gn_b.rearrange("(k p t) -> p k t", p=P, t=PACK))
         skip_bf = consts.tile([P, 1], BF16, name="skip_bf")
         nc.scalar.dma_start(out=skip_bf[:], in_=skip_scale.partition_broadcast(P))
 
-        load_h(0, 0, 0)
-        load_h(0, 0, 1)
-        w_raw = consts.tile([P, D_MODEL // P, CHANNELS], BF16, name="w_raw")
-        nc.sync.dma_start(out=w_raw[:], in_=W_out.rearrange("(m p) c -> p m c", p=P))
+        load_h(0, 0, 0, 2)
+        load_h(0, 0, 1, 2)
         load_h(0, 1, 0)
         load_h(0, 1, 1)
+        w_raw = consts.tile([P, D_MODEL // P, CHANNELS], BF16, name="w_raw")
+        nc.sync.dma_start(out=w_raw[:], in_=W_out.rearrange("(m p) c -> p m c", p=P))
+        load_h(1, 0, 0)
+        load_h(1, 0, 1)
         load_x(0, 0)
         load_x(0, 1)
-        for b in range(1, RESIDENT):
+        load_h(1, 1, 0)
+        load_h(1, 1, 1)
+        load_x(1, 0)
+        load_x(1, 1)
+        for b in (2, 3):
             for k in range(PASSES):
                 for half in range(HALVES):
                     load_h(b, k, half)
 
-        gn_ps = tp_psum.tile([P, HALF_TOKENS], BF16, name="tp")
-        for t in range(PACK):
-            nc.tensor.transpose(gn_ps[:, t * P : (t + 1) * P], gn_rows[:, t :: PACK], ident[:])
-        gn_cols = consts.tile([P, 2 * PASSES, PACK], F32, name="gn_cols")
-        nc.vector.tensor_copy(
-            out=gn_cols[:], in_=gn_ps[:, 0 : PACK * P].rearrange("p (t m) -> p m t", t=PACK)[:, 0 : 2 * PASSES, :]
-        )
+        ident = consts.tile([P, P], BF16, name="ident")
+        make_identity(nc, ident[:])
+        ident_f = consts.tile([P, P], F32, name="ident_f")
+        make_identity(nc, ident_f[:])
+        warm = consts.tile([P, 1], F32, name="warm")
+        nc.vector.memset(warm[:], 1.0)
+        nc.scalar.activation(out=warm[:], in_=warm[:], func=ACT.Sqrt)
+        neg_col = consts.tile([P, 2], BF16, name="neg_col")
+        nc.vector.memset(neg_col[:], -1.0)
+        mean_mat = consts.tile([P, GROUPS_PER_PASS, P], F32, name="mean_mat")
+        nc.vector.memset(mean_mat[:], 0.0)
+        for g in range(GROUPS_PER_PASS):
+            nc.vector.memset(mean_mat[:, g, g * GROUP_PARTS : (g + 1) * GROUP_PARTS], 1.0 / (SEQ * GROUP))
         skip_f = consts.tile([P, 1], F32, name="skip_f")
-        nc.vector.tensor_copy(out=skip_f[:], in_=skip_bf[:])
 
         parts = {}
-        stat_banks = {}
+        banks = {}
+        n_cols = {}
         scale_bias = {}
+        SUMS = 16
 
-        def start_stats(b, k):
-            parts[(b, k)] = stat_pool.tile([P, 2, 8], F32, name="parts")
-            stat_banks[(b, k)] = stat_psum.tile([P, 16], F32, name="stat_bank")
+        def start_stats(b, k, n_squares):
+            parts[(b, k)] = stat_pool.tile([P, GROUPS_PER_PASS, 8], F32, name="parts")
+            banks[(b, k)] = stat_psum.tile([P, 32], F32, name="stat_bank")
+            n_cols[(b, k)] = 1 + n_squares
 
-        def square_sums(b, k, half):
-            for g in range(GROUPS_PER_PASS):
-                squares = work.tile([P, HALF_ROWS, GROUP], BF16, name="squares")
-                nc.scalar.activation(
-                    out=squares[:],
-                    in_=h_tiles[(b, k, half)][:, :, g * GROUP : (g + 1) * GROUP],
-                    func=ACT.Square,
-                    accum_out=parts[(b, k)][:, 1, g * HALVES + half : g * HALVES + half + 1],
-                )
+        def square_scalar(b, k, half, rows, g, col):
+            squares = junk_pool.tile([P, HALF_ROWS, GROUP], BF16, name="squares")
+            n = rows.stop - rows.start
+            nc.scalar.activation(
+                out=squares[:, 0:n, :],
+                in_=h_tiles[(b, k, half)][:, rows, g * GROUP : (g + 1) * GROUP],
+                func=ACT.Square,
+                accum_out=parts[(b, k)][:, g, col : col + 1],
+            )
 
-        def channel_sums(b, k, half):
+        def square_vector(b, k, half, rows, g, col):
+            squares_v = junk_pool.tile([P, 2, GROUP], BF16, name="squares_v")
+            x_in = h_tiles[(b, k, half)][:, rows, g * GROUP : (g + 1) * GROUP]
+            nc.vector.scalar_tensor_tensor(
+                out=squares_v[:], in0=x_in, scalar=1.0, in1=x_in, op0=ALU.mult, op1=ALU.mult,
+                accum_out=parts[(b, k)][:, g, col : col + 1],
+            )
+
+        def channel_sums(b, k, half, rows, seg, n_seg):
             for t in range(PACK):
-                col = t * HALVES + half
-                for r in range(HALF_ROWS):
+                col = t * n_seg + seg
+                for r in range(rows.start, rows.stop):
                     nc.tensor.matmul(
-                        out=stat_banks[(b, k)][:, col : col + 1],
+                        out=banks[(b, k)][:, col : col + 1],
                         lhsT=h_tiles[(b, k, half)][:, r, t * P : (t + 1) * P],
-                        rhs=ones_col[:, 0:1],
-                        start=(r == 0),
-                        stop=(r == HALF_ROWS - 1),
+                        rhs=neg_col[:, 0:1],
+                        start=(r == rows.start),
+                        stop=(r == rows.stop - 1),
                     )
 
-        def finish_stats(b, k):
-            bank = stat_banks[(b, k)]
-            n_sum = PACK * HALVES
-            n_part = GROUPS_PER_PASS * HALVES
+        def gram(grams, b, k, half, rows, first, last):
+            for g in range(GROUPS_PER_PASS):
+                for r in range(rows.start, rows.stop):
+                    for j in range(GROUP // P):
+                        block = h_tiles[(b, k, half)][:, r, g * GROUP + j * P : g * GROUP + (j + 1) * P]
+                        nc.tensor.matmul(
+                            out=grams[g][:, 0, 0:P],
+                            lhsT=block,
+                            rhs=block,
+                            start=(first and r == rows.start and j == 0),
+                            stop=(last and r == rows.stop - 1 and j == GROUP // P - 1),
+                        )
+
+        def gram_trace(grams, b, k, col):
+            for g in range(GROUPS_PER_PASS):
+                diag = junk_pool.tile([P, P], F32, name="diag")
+                nc.vector.scalar_tensor_tensor(
+                    out=diag[:], in0=grams[g][:, 0, 0:P], scalar=1.0, in1=ident_f[:], op0=ALU.mult, op1=ALU.mult,
+                    accum_out=parts[(b, k)][:, g, col : col + 1],
+                )
+
+        def stat_reduce(b, k, n_seg):
             nc.vector.tensor_reduce(
-                out=parts[(b, k)][:, 0, 0:n_part].rearrange("p (g s) -> p g s", g=GROUPS_PER_PASS),
-                in_=bank[:, 0:n_sum].rearrange("p (g j s) -> p g s j", g=GROUPS_PER_PASS, j=TILES_PER_GROUP),
+                out=parts[(b, k)][:, :, 0:1].rearrange("p g o -> p (g o)"),
+                in_=banks[(b, k)][:, 0 : PACK * n_seg].rearrange("p (g s) -> p g s", g=GROUPS_PER_PASS),
                 axis=AXIS.X,
                 op=ALU.add,
             )
-            sums = bank[:, n_sum : n_sum + 2 * HALVES].rearrange("p (a s) -> p a s", a=2)
+
+        def stat_total(b, k):
+            n = n_cols[(b, k)]
             for g in range(GROUPS_PER_PASS):
                 nc.tensor.matmul(
-                    out=sums,
+                    out=banks[(b, k)][:, SUMS : SUMS + n],
                     lhsT=mean_mat[:, g, :],
-                    rhs=parts[(b, k)][:, :, g * HALVES : (g + 1) * HALVES],
+                    rhs=parts[(b, k)][:, g, 0:n],
                     start=(g == 0),
                     stop=(g == GROUPS_PER_PASS - 1),
                 )
-            both = stat_pool.tile([P, 2], F32, name="both")
-            nc.vector.tensor_reduce(out=both[:], in_=sums, axis=AXIS.X, op=ALU.add)
-            neg_mean = both[:, 0:1]
-            ex2 = both[:, 1:2]
-            mean_sq = stat_pool.tile([P, 1], F32, name="mean_sq")
-            nc.scalar.activation(out=mean_sq[:], in_=neg_mean, func=ACT.Square)
-            var_eps = stat_pool.tile([P, 1], F32, name="var_eps")
+
+        std_tiles = {}
+        var_tiles = {}
+
+        def stat_square(b, k):
+            bank = banks[(b, k)]
+            n = n_cols[(b, k)]
+            ex2 = stat_pool.tile([P, 1], F32, name="ex2")
+            nc.vector.tensor_reduce(out=ex2[:], in_=bank[:, SUMS + 1 : SUMS + n], axis=AXIS.X, op=ALU.add)
+            neg_var = stat_pool.tile([P, 1], F32, name="neg_var")
             nc.vector.scalar_tensor_tensor(
-                out=var_eps[:], in0=ex2, scalar=EPS, in1=mean_sq[:], op0=ALU.add, op1=ALU.subtract
+                out=neg_var[:],
+                in0=bank[:, SUMS : SUMS + 1],
+                scalar=bank[:, SUMS : SUMS + 1],
+                in1=ex2[:],
+                op0=ALU.mult,
+                op1=ALU.subtract,
             )
+            var_tiles[(b, k)] = neg_var
+
+        def stat_std(b, k):
             std = stat_pool.tile([P, 1], F32, name="std")
-            nc.scalar.activation(out=std[:], in_=var_eps[:], func=ACT.Sqrt)
+            nc.scalar.activation(out=std[:], in_=var_tiles[(b, k)][:], func=ACT.Sqrt, scale=-1.0, bias=EPS)
+            std_tiles[(b, k)] = std
+
+        def stat_affine(b, k):
             rstd = stat_pool.tile([P, 1], F32, name="rstd")
-            nc.vector.reciprocal(out=rstd[:], in_=std[:])
+            nc.vector.reciprocal(out=rstd[:], in_=std_tiles[(b, k)][:])
             scale = stat_pool.tile([P, PACK], F32, name="scale")
-            nc.vector.tensor_scalar(out=scale[:], in0=gn_cols[:, k, :], scalar1=rstd[:, 0:1], scalar2=None, op0=ALU.mult)
+            nc.vector.tensor_scalar(out=scale[:], in0=gnw[:, k, :], scalar1=rstd[:, 0:1], scalar2=None, op0=ALU.mult)
             bias = stat_pool.tile([P, PACK], F32, name="bias")
             nc.vector.scalar_tensor_tensor(
-                out=bias[:], in0=scale[:], scalar=neg_mean, in1=gn_cols[:, PASSES + k, :], op0=ALU.mult, op1=ALU.add
+                out=bias[:],
+                in0=scale[:],
+                scalar=banks[(b, k)][:, SUMS : SUMS + 1],
+                in1=gnb[:, k, :],
+                op0=ALU.mult,
+                op1=ALU.add,
             )
             scale_bias[(b, k)] = (scale, bias)
 
@@ -186,111 +240,218 @@ def tile_mlstmblock_pb_t_kernel(tc, h_attn, gn_w, gn_b, W_out, x, skip_scale, ou
         w_codes = consts.tile([P, PASSES * D_MODEL], U32, name="w_codes", align_bytes=64)
         w_scales = consts.tile([P, PASSES * D_MODEL], U8, name="w_scales", align_bytes=64)
 
-        def prepare_w():
+        def transpose_w():
             for k in range(PASSES):
-                w_ps = tp_psum.tile([P, PACK * D_MODEL], BF16, name="tp")
-                for t in range(PACK):
+                w_ps = tp_psum.tile([P, 2, D_MODEL], F32, name="tp")
+                for u in range(2):
                     for m in range(D_MODEL // P):
+                        words = w_raw[:, m, :].bitcast(F32)
                         nc.tensor.transpose(
-                            w_ps[:, t * D_MODEL + m * P : t * D_MODEL + (m + 1) * P], w_raw[:, m, k * K_PASS + t : (k + 1) * K_PASS : PACK], ident[:]
+                            w_ps[:, u, m * P : (m + 1) * P],
+                            words[:, k * 2 * P + u : (k + 1) * 2 * P : 2],
+                            ident_f[:],
                         )
-                nc.vector.tensor_copy(out=w_grouped[:, k], in_=w_ps[:].rearrange("p (t n) -> p n t", t=PACK))
+                nc.scalar.copy(
+                    out=w_grouped[:, k].rearrange("p n t -> p (n t)").bitcast(F32).rearrange("p (n u) -> p n u", u=2),
+                    in_=w_ps[:].rearrange("p u n -> p n u"),
+                )
+
+        def quantise_w():
             nc.vector.quantize_mx(
                 out=w_codes[:].bitcast(FP8X4),
                 scales=w_scales[:],
                 in_=w_grouped[:].rearrange("p k n t -> p (k n t)"),
             )
 
+        units = [(0, k, half) for k in range(PASSES) for half in range(HALVES)]
+        units += [(b, k, half) for b in range(1, BATCH) for half in range(HALVES) for k in range(PASSES)]
+        N = len(units)
+        tps = {}
+        planes = {}
+        grouped = {}
         h_codes = {}
+        accs = {}
+        results = {}
 
-        def normalise(b, k, half):
-            scale, bias = scale_bias[(b, k)]
-            planes = work.tile([P, PACK, HALF_TOKENS], BF16, name="planes")
-            on_scalar = 1 + half
-            for t in range(PACK):
+        def on_vector(u):
+            if units[u][0] == BATCH - 1:
+                return 2 if u == N - 1 else (1 if u % 2 else 0)
+            return 2 + u % 2
+
+        def transposes(u, ts=range(PACK)):
+            b, k, half = units[u]
+            for t in ts:
                 tp = tp_psum.tile([P, HALF_TOKENS], BF16, name="tp")
                 for r in range(HALF_ROWS):
                     nc.tensor.transpose(tp[:, r * P : (r + 1) * P], h_tiles[(b, k, half)][:, r, t::PACK], ident[:])
-                if t >= PACK - on_scalar:
-                    nc.scalar.activation(
-                        out=planes[:, t, :], in_=tp[:], func=ACT.Identity, scale=scale[:, t : t + 1], bias=bias[:, t : t + 1]
-                    )
-                else:
+                tps[(u, t)] = tp
+
+        def normalise(u):
+            b, k, half = units[u]
+            scale, bias = scale_bias[(b, k)]
+            plane = work.tile([P, PACK, HALF_TOKENS], BF16, name="plane")
+            planes[u] = plane
+            for t in range(PACK):
+                if t < on_vector(u):
                     nc.vector.tensor_scalar(
-                        out=planes[:, t, :],
-                        in0=tp[:],
+                        out=plane[:, t, :],
+                        in0=tps[(u, t)][:],
                         scalar1=scale[:, t : t + 1],
                         scalar2=bias[:, t : t + 1],
                         op0=ALU.mult,
                         op1=ALU.add,
                     )
-            return planes
+                else:
+                    nc.scalar.activation(
+                        out=plane[:, t, :],
+                        in_=tps[(u, t)][:],
+                        func=ACT.Identity,
+                        scale=scale[:, t : t + 1],
+                        bias=bias[:, t : t + 1],
+                    )
 
-        def quantise(b, k, half, planes):
-            grouped = work.tile([P, HALF_TOKENS, PACK], BF16, name="grouped", align_bytes=64)
+        def regroup(u):
+            grp = work.tile([P, HALF_TOKENS, PACK], BF16, name="grp", align_bytes=64)
             nc.vector.tensor_copy(
-                out=grouped[:].rearrange("p (c i) t -> p c t i", i=4),
-                in_=planes[:].rearrange("p t (c i) -> p c t i", i=4),
+                out=grp[:].rearrange("p (c i) t -> p c t i", i=4),
+                in_=planes[u][:].rearrange("p t (c i) -> p c t i", i=4),
             )
+            grouped[u] = grp
+
+        def quantise(u):
+            b, k, half = units[u]
             codes = codes_pool.tile([P, HALF_TOKENS], U32, name="codes%d%d" % (k, half), align_bytes=64)
             scales = codes_pool.tile([P, HALF_TOKENS], U8, name="scales%d%d" % (k, half), align_bytes=64)
             nc.vector.quantize_mx(
-                out=codes[:].bitcast(FP8X4), scales=scales[:], in_=grouped[:].rearrange("p r t -> p (r t)")
+                out=codes[:].bitcast(FP8X4), scales=scales[:], in_=grouped[u][:].rearrange("p r t -> p (r t)")
             )
             h_codes[(k, half)] = (codes, scales)
 
-        def project(b, half):
-            result = work.tile([P, HALF_ROWS, D_MODEL], F32, name="result")
-            for pair in range(HALF_ROWS // ROWS_PER_BANK):
-                acc = mm_psum.tile([P, ROWS_PER_BANK, D_MODEL], F32, name="acc")
-                for s in range(ROWS_PER_BANK):
-                    r = ROWS_PER_BANK * pair + s
-                    for k in range(PASSES):
-                        codes, scales = h_codes[(k, half)]
-                        nc.tensor.matmul_mx(
-                            out=acc[:, s, :],
-                            lhsT=codes[:, r * P : (r + 1) * P].bitcast(FP8X4),
-                            lhsT_scale=scales[:, r * P : (r + 1) * P],
-                            rhs=w_codes[:, k * D_MODEL : (k + 1) * D_MODEL].bitcast(FP8X4),
-                            rhs_scale=w_scales[:, k * D_MODEL : (k + 1) * D_MODEL],
-                            start=(k == 0),
-                            stop=(k == PASSES - 1),
-                        )
-                rows = slice(ROWS_PER_BANK * pair, ROWS_PER_BANK * (pair + 1))
-                nc.vector.scalar_tensor_tensor(
-                    out=result[:, rows, :].rearrange("p s d -> p (s d)"),
-                    in0=x_tiles[(b, half)][:, rows, :].rearrange("p s d -> p (s d)"),
-                    scalar=skip_f[:, 0:1],
-                    in1=acc[:].rearrange("p s d -> p (s d)"),
-                    op0=ALU.mult,
-                    op1=ALU.add,
-                )
-            nc.sync.dma_start(out=out_view[b, :, half * HALF_ROWS : (half + 1) * HALF_ROWS, :], in_=result[:])
+        def multiply(b, half, pair):
+            acc = mm_psum.tile([P, ROWS_PER_BANK, D_MODEL], F32, name="acc")
+            for s in range(ROWS_PER_BANK):
+                r = ROWS_PER_BANK * pair + s
+                for k in range(PASSES):
+                    codes, scales = h_codes[(k, half)]
+                    nc.tensor.matmul_mx(
+                        out=acc[:, s, :],
+                        lhsT=codes[:, r * P : (r + 1) * P].bitcast(FP8X4),
+                        lhsT_scale=scales[:, r * P : (r + 1) * P],
+                        rhs=w_codes[:, k * D_MODEL : (k + 1) * D_MODEL].bitcast(FP8X4),
+                        rhs_scale=w_scales[:, k * D_MODEL : (k + 1) * D_MODEL],
+                        start=(k == 0),
+                        stop=(k == PASSES - 1),
+                    )
+            accs[(b, half, pair)] = acc
 
-        for k in range(PASSES):
-            start_stats(0, k)
-            for half in range(HALVES):
-                square_sums(0, k, half)
-                channel_sums(0, k, half)
-            finish_stats(0, k)
-            if k == 0:
-                prepare_w()
+        def add_skip(b, half, pair):
+            if pair == 0:
+                results[(b, half)] = work.tile([P, HALF_ROWS, D_MODEL], F32, name="result")
+            rows = slice(ROWS_PER_BANK * pair, ROWS_PER_BANK * (pair + 1))
+            nc.vector.scalar_tensor_tensor(
+                out=results[(b, half)][:, rows, :].rearrange("p s d -> p (s d)"),
+                in0=x_tiles[(b, half)][:, rows, :].rearrange("p s d -> p (s d)"),
+                scalar=skip_f[:, 0:1],
+                in1=accs[(b, half, pair)][:].rearrange("p s d -> p (s d)"),
+                op0=ALU.mult,
+                op1=ALU.add,
+            )
 
-        for b in range(BATCH):
-            for k in range(PASSES):
-                for half in range(HALVES):
-                    planes = normalise(b, k, half)
-                    if b + 1 < BATCH:
-                        if half == 0:
-                            start_stats(b + 1, k)
-                        square_sums(b + 1, k, half)
-                        channel_sums(b + 1, k, half)
-                    quantise(b, k, half, planes)
-                    if b + 1 < BATCH and half == HALVES - 1:
-                        finish_stats(b + 1, k)
-                    if k == PASSES - 1:
-                        project(b, half)
-                    if b + RESIDENT < BATCH:
-                        load_h(b + RESIDENT, k, half)
-                    if b + 1 < BATCH and k == 0:
-                        load_x(b + 1, half)
+        def store(b, half, rows):
+            r0 = half * HALF_ROWS
+            nc.sync.dma_start(
+                out=out_view[b, :, r0 + rows.start : r0 + rows.stop, :], in_=results[(b, half)][:, rows, :]
+            )
+
+        start_stats(0, 0, CHUNKS + 1)
+        grams = [mm_psum.tile([P, ROWS_PER_BANK, D_MODEL], F32, name="acc") for g in range(GROUPS_PER_PASS)]
+        for c in range(CHUNKS):
+            half, r0 = divmod(c * CHUNK_ROWS, HALF_ROWS)
+            square_scalar(0, 0, half, slice(r0, r0 + 2), 0, 1 + c)
+            square_vector(0, 0, half, slice(r0, r0 + 2), 1, 1 + c)
+            gram(grams, 0, 0, half, slice(r0 + 2, r0 + 4), c == 0, c == CHUNKS - 1)
+            channel_sums(0, 0, half, slice(r0, r0 + CHUNK_ROWS), c, CHUNKS)
+            if 1 <= c < CHUNKS - 1:
+                transposes(0, [c - 1])
+        gram_trace(grams, 0, 0, 1 + CHUNKS)
+        stat_reduce(0, 0, CHUNKS)
+        stat_total(0, 0)
+        stat_square(0, 0)
+        stat_std(0, 0)
+        stat_affine(0, 0)
+        transposes(0, [2, 3])
+        nc.vector.tensor_copy(out=skip_f[:], in_=skip_bf[:])
+        start_stats(0, 1, 1)
+        grams = [mm_psum.tile([P, ROWS_PER_BANK, D_MODEL], F32, name="acc") for g in range(GROUPS_PER_PASS)]
+        gram(grams, 0, 1, 0, slice(0, HALF_ROWS), True, False)
+        channel_sums(0, 1, 0, slice(0, HALF_ROWS), 0, HALVES)
+
+        ready = []
+        complete = []
+        deviations = []
+        for u in range(N + 2):
+            now, ready = ready, []
+            done, complete = complete, []
+            if 1 <= u <= N:
+                regroup(u - 1)
+            for b, k in done:
+                stat_reduce(b, k, HALVES)
+                stat_total(b, k)
+            for bk in deviations:
+                stat_affine(*bk)
+            deviations = list(done)
+            for b, half in now:
+                add_skip(b, half, 0)
+                multiply(b, half, 2)
+                add_skip(b, half, 1)
+                multiply(b, half, 3)
+            if u < N:
+                normalise(u)
+            if u == 1:
+                transpose_w()
+            for bk in done:
+                stat_square(*bk)
+            if u < N - UNITS_PER_BATCH:
+                b = u // UNITS_PER_BATCH + 1
+                k, half = divmod(u % UNITS_PER_BATCH, HALVES)
+                if half == 0:
+                    start_stats(b, k, HALVES)
+                square_scalar(b, k, half, slice(0, HALF_ROWS), 0, 1 + half)
+            for bk in done:
+                stat_std(*bk)
+            if u < N - UNITS_PER_BATCH:
+                square_scalar(b, k, half, slice(0, HALF_ROWS), 1, 1 + half)
+                if half == 1:
+                    complete.append((b, k))
+            for b, half in now:
+                add_skip(b, half, 2)
+                add_skip(b, half, 3)
+                store(b, half, slice(0, HALF_ROWS))
+                if 2 * b + half + 4 < 2 * BATCH:
+                    load_x(b + 2, half)
+            if u == 2:
+                quantise_w()
+            if 1 <= u <= N:
+                quantise(u - 1)
+            if u == 1:
+                gram_trace(grams, 0, 1, 1)
+                stat_reduce(0, 1, HALVES)
+                stat_total(0, 1)
+                stat_square(0, 1)
+                stat_std(0, 1)
+                deviations.append((0, 1))
+            if u + 1 < N:
+                transposes(u + 1)
+            if u == 0:
+                gram(grams, 0, 1, 1, slice(0, HALF_ROWS), False, True)
+                channel_sums(0, 1, 1, slice(0, HALF_ROWS), 1, HALVES)
+            if u < N - UNITS_PER_BATCH:
+                b = u // UNITS_PER_BATCH + 1
+                k, half = divmod(u % UNITS_PER_BATCH, HALVES)
+                channel_sums(b, k, half, slice(0, HALF_ROWS), half, HALVES)
+            if 1 <= u <= N:
+                b, k, half = units[u - 1]
+                if k == PASSES - 1:
+                    ready.append((b, half))
+                    multiply(b, half, 0)
+                    multiply(b, half, 1)

@@ -274,61 +274,84 @@ def tile_mlstmblock_pb_t_kernel(tc, h_attn, gn_w, gn_b, W_out, x, skip_scale, ou
         results = {}
 
         def on_vector(u):
-            if units[u][0] == BATCH - 1:
-                return 2 if u == N - 1 else (1 if u % 2 else 0)
-            return 2 + u % 2
+            return 2 if units[u][0] < BATCH - 1 or u == N - 1 else 0
 
-        def transposes(u, ts=range(PACK)):
+        def bank_order(u):
+            if on_vector(u) == 0:
+                return [(1, pair, th) for th in range(2) for pair in range(2)]
+            return [(0, 0, 0), (1, 1, 0), (0, 1, 0), (1, 1, 1)]
+
+        def transposes(u, which=range(4)):
             b, k, half = units[u]
-            for t in ts:
-                tp = tp_psum.tile([P, HALF_TOKENS], BF16, name="tp")
-                for r in range(HALF_ROWS):
-                    nc.tensor.transpose(tp[:, r * P : (r + 1) * P], h_tiles[(b, k, half)][:, r, t::PACK], ident[:])
-                tps[(u, t)] = tp
+            h_tile = h_tiles[(b, k, half)]
+            for key in [bank_order(u)[i] for i in which]:
+                as_words, j, th = key
+                if as_words:
+                    tp = tp_psum.tile([P, HALF_TOKENS // 2], F32, name="tp")
+                    for r in range(HALF_ROWS // 2):
+                        words = h_tile[:, th * HALF_ROWS // 2 + r, :].bitcast(F32)
+                        nc.tensor.transpose(tp[:, r * P : (r + 1) * P], words[:, j::2], ident_f[:])
+                else:
+                    tp = tp_psum.tile([P, HALF_TOKENS], BF16, name="tp")
+                    for r in range(HALF_ROWS):
+                        nc.tensor.transpose(tp[:, r * P : (r + 1) * P], h_tile[:, r, j::PACK], ident[:])
+                tps[(u, key)] = tp
 
         def normalise(u):
             b, k, half = units[u]
             scale, bias = scale_bias[(b, k)]
             plane = work.tile([P, PACK, HALF_TOKENS], BF16, name="plane")
             planes[u] = plane
-            for t in range(PACK):
-                if t < on_vector(u):
+            for key in bank_order(u):
+                as_words, j, th = key
+                tp = tps[(u, key)]
+                if as_words:
+                    n = HALF_TOKENS // 2
+                    for e in range(2):
+                        t = 2 * j + e
+                        nc.scalar.activation(
+                            out=plane[:, t, th * n : (th + 1) * n],
+                            in_=tp[:].bitcast(BF16).rearrange("p (i e) -> p e i", e=2)[:, e, :],
+                            func=ACT.Identity,
+                            scale=scale[:, t : t + 1],
+                            bias=bias[:, t : t + 1],
+                        )
+                else:
                     nc.vector.tensor_scalar(
-                        out=plane[:, t, :],
-                        in0=tps[(u, t)][:],
-                        scalar1=scale[:, t : t + 1],
-                        scalar2=bias[:, t : t + 1],
+                        out=plane[:, j, :],
+                        in0=tp[:],
+                        scalar1=scale[:, j : j + 1],
+                        scalar2=bias[:, j : j + 1],
                         op0=ALU.mult,
                         op1=ALU.add,
                     )
-                else:
-                    nc.scalar.activation(
-                        out=plane[:, t, :],
-                        in_=tps[(u, t)][:],
-                        func=ACT.Identity,
-                        scale=scale[:, t : t + 1],
-                        bias=bias[:, t : t + 1],
-                    )
 
-        def regroup(u):
-            grp = work.tile([P, HALF_TOKENS, PACK], BF16, name="grp", align_bytes=64)
-            nc.vector.tensor_copy(
-                out=grp[:].rearrange("p (c i) t -> p c t i", i=4),
-                in_=planes[u][:].rearrange("p t (c i) -> p c t i", i=4),
+        def regroup(copy, u, t0, t1):
+            if u not in grouped:
+                grouped[u] = work.tile([P, HALF_TOKENS, PACK], BF16, name="grp", align_bytes=64)
+            copy(
+                out=grouped[u][:, t0:t1, :].rearrange("p (c i) t -> p c t i", i=4),
+                in_=planes[u][:, :, t0:t1].rearrange("p t (c i) -> p c t i", i=4),
             )
-            grouped[u] = grp
 
-        def quantise(u):
+        def quantise(u, t0, t1):
             b, k, half = units[u]
-            codes = codes_pool.tile([P, HALF_TOKENS], U32, name="codes%d%d" % (k, half), align_bytes=64)
-            scales = codes_pool.tile([P, HALF_TOKENS], U8, name="scales%d%d" % (k, half), align_bytes=64)
+            if t0 == 0:
+                codes = codes_pool.tile([P, HALF_TOKENS], U32, name="codes%d%d" % (k, half), align_bytes=64)
+                scales = codes_pool.tile([P, HALF_TOKENS], U8, name="scales%d%d" % (k, half), align_bytes=64)
+                h_codes[(k, half)] = (codes, scales)
+            codes, scales = h_codes[(k, half)]
             nc.vector.quantize_mx(
-                out=codes[:].bitcast(FP8X4), scales=scales[:], in_=grouped[u][:].rearrange("p r t -> p (r t)")
+                out=codes[:, t0:t1].bitcast(FP8X4),
+                scales=scales[:, t0:t1],
+                in_=grouped[u][:, t0:t1, :].rearrange("p r t -> p (r t)"),
             )
-            h_codes[(k, half)] = (codes, scales)
 
         def multiply(b, half, pair):
-            acc = mm_psum.tile([P, ROWS_PER_BANK, D_MODEL], F32, name="acc")
+            if (b, half) == (BATCH - 1, HALVES - 1) and pair >= 2:
+                acc = tp_psum.tile([P, ROWS_PER_BANK, D_MODEL], F32, name="tp")
+            else:
+                acc = mm_psum.tile([P, ROWS_PER_BANK, D_MODEL], F32, name="acc")
             for s in range(ROWS_PER_BANK):
                 r = ROWS_PER_BANK * pair + s
                 for k in range(PASSES):
@@ -389,11 +412,11 @@ def tile_mlstmblock_pb_t_kernel(tc, h_attn, gn_w, gn_b, W_out, x, skip_scale, ou
         ready = []
         complete = []
         deviations = []
-        for u in range(N + 2):
+        for u in range(N):
             now, ready = ready, []
             done, complete = complete, []
-            if 1 <= u <= N:
-                regroup(u - 1)
+            if 1 <= u < N:
+                regroup(nc.vector.tensor_copy, u - 1, 0, HALF_TOKENS)
             for b, k in done:
                 stat_reduce(b, k, HALVES)
                 stat_total(b, k)
@@ -405,8 +428,7 @@ def tile_mlstmblock_pb_t_kernel(tc, h_attn, gn_w, gn_b, W_out, x, skip_scale, ou
                 multiply(b, half, 2)
                 add_skip(b, half, 1)
                 multiply(b, half, 3)
-            if u < N:
-                normalise(u)
+            normalise(u)
             if u == 1:
                 transpose_w()
             for bk in done:
@@ -431,8 +453,8 @@ def tile_mlstmblock_pb_t_kernel(tc, h_attn, gn_w, gn_b, W_out, x, skip_scale, ou
                     load_x(b + 2, half)
             if u == 2:
                 quantise_w()
-            if 1 <= u <= N:
-                quantise(u - 1)
+            if 1 <= u < N:
+                quantise(u - 1, 0, HALF_TOKENS)
             if u == 1:
                 gram_trace(grams, 0, 1, 1)
                 stat_reduce(0, 1, HALVES)
@@ -449,9 +471,26 @@ def tile_mlstmblock_pb_t_kernel(tc, h_attn, gn_w, gn_b, W_out, x, skip_scale, ou
                 b = u // UNITS_PER_BATCH + 1
                 k, half = divmod(u % UNITS_PER_BATCH, HALVES)
                 channel_sums(b, k, half, slice(0, HALF_ROWS), half, HALVES)
-            if 1 <= u <= N:
+            if 1 <= u < N:
                 b, k, half = units[u - 1]
                 if k == PASSES - 1:
                     ready.append((b, half))
                     multiply(b, half, 0)
                     multiply(b, half, 1)
+        u = N - 1
+        b, k, half = units[u]
+        regroup(nc.scalar.copy, u, 512, 768)
+        regroup(nc.vector.tensor_copy, u, 0, 512)
+        regroup(nc.vector.tensor_copy, u, 768, 1024)
+        quantise(u, 0, 512)
+        multiply(b, half, 0)
+        multiply(b, half, 1)
+        quantise(u, 512, 1024)
+        multiply(b, half, 2)
+        multiply(b, half, 3)
+        add_skip(b, half, 0)
+        add_skip(b, half, 1)
+        store(b, half, slice(0, HALF_ROWS // 2))
+        add_skip(b, half, 2)
+        add_skip(b, half, 3)
+        store(b, half, slice(HALF_ROWS // 2, HALF_ROWS))

@@ -137,10 +137,11 @@ def tile_mlstmblock_pb_t_kernel(tc, h_attn, gn_w, gn_b, W_out, x, skip_scale, ou
             )
 
         def square_vector(b, k, half, rows, g, col):
-            squares_v = junk_pool.tile([P, 2, GROUP], BF16, name="squares_v")
+            squares_v = junk_pool.tile([P, HALF_ROWS, GROUP], BF16, name="squares_v")
+            n = rows.stop - rows.start
             x_in = h_tiles[(b, k, half)][:, rows, g * GROUP : (g + 1) * GROUP]
             nc.vector.scalar_tensor_tensor(
-                out=squares_v[:], in0=x_in, scalar=1.0, in1=x_in, op0=ALU.mult, op1=ALU.mult,
+                out=squares_v[:, 0:n, :], in0=x_in, scalar=1.0, in1=x_in, op0=ALU.mult, op1=ALU.mult,
                 accum_out=parts[(b, k)][:, g, col : col + 1],
             )
 
@@ -274,7 +275,7 @@ def tile_mlstmblock_pb_t_kernel(tc, h_attn, gn_w, gn_b, W_out, x, skip_scale, ou
         results = {}
 
         def on_vector(u):
-            return 2 if units[u][0] < BATCH - 1 or u == N - 1 else 0
+            return 2 if u < 12 or u == N - 1 else 0
 
         def bank_order(u):
             if on_vector(u) == 0:
@@ -390,23 +391,24 @@ def tile_mlstmblock_pb_t_kernel(tc, h_attn, gn_w, gn_b, W_out, x, skip_scale, ou
         grams = [mm_psum.tile([P, ROWS_PER_BANK, D_MODEL], F32, name="acc") for g in range(GROUPS_PER_PASS)]
         for c in range(CHUNKS):
             half, r0 = divmod(c * CHUNK_ROWS, HALF_ROWS)
-            square_scalar(0, 0, half, slice(r0, r0 + 2), 0, 1 + c)
-            square_vector(0, 0, half, slice(r0, r0 + 2), 1, 1 + c)
-            gram(grams, 0, 0, half, slice(r0 + 2, r0 + 4), c == 0, c == CHUNKS - 1)
-            channel_sums(0, 0, half, slice(r0, r0 + CHUNK_ROWS), c, CHUNKS)
+            r1 = r0 + CHUNK_ROWS
+            square_scalar(0, 0, half, slice(r0, r1 - 1), 0, 1 + c)
+            square_vector(0, 0, half, slice(r0, r1 - 1), 1, 1 + c)
+            gram(grams, 0, 0, half, slice(r1 - 1, r1), c == 0, c == CHUNKS - 1)
+            channel_sums(0, 0, half, slice(r0, r1), c, CHUNKS)
             if 1 <= c < CHUNKS - 1:
                 transposes(0, [c - 1])
         gram_trace(grams, 0, 0, 1 + CHUNKS)
         stat_reduce(0, 0, CHUNKS)
         stat_total(0, 0)
+        start_stats(0, 1, HALVES)
+        square_vector(0, 1, 0, slice(0, HALF_ROWS), 1, 1)
         stat_square(0, 0)
+        square_scalar(0, 1, 0, slice(0, HALF_ROWS), 0, 1)
         stat_std(0, 0)
         stat_affine(0, 0)
         transposes(0, [2, 3])
         nc.vector.tensor_copy(out=skip_f[:], in_=skip_bf[:])
-        start_stats(0, 1, 1)
-        grams = [mm_psum.tile([P, ROWS_PER_BANK, D_MODEL], F32, name="acc") for g in range(GROUPS_PER_PASS)]
-        gram(grams, 0, 1, 0, slice(0, HALF_ROWS), True, False)
         channel_sums(0, 1, 0, slice(0, HALF_ROWS), 0, HALVES)
 
         ready = []
@@ -429,7 +431,13 @@ def tile_mlstmblock_pb_t_kernel(tc, h_attn, gn_w, gn_b, W_out, x, skip_scale, ou
                 add_skip(b, half, 1)
                 multiply(b, half, 3)
             normalise(u)
+            if u == 0:
+                for g in range(GROUPS_PER_PASS):
+                    square_vector(0, 1, 1, slice(0, HALF_ROWS), g, 2)
             if u == 1:
+                stat_square(0, 1)
+                stat_std(0, 1)
+                deviations.append((0, 1))
                 transpose_w()
             for bk in done:
                 stat_square(*bk)
@@ -437,12 +445,17 @@ def tile_mlstmblock_pb_t_kernel(tc, h_attn, gn_w, gn_b, W_out, x, skip_scale, ou
                 b = u // UNITS_PER_BATCH + 1
                 k, half = divmod(u % UNITS_PER_BATCH, HALVES)
                 if half == 0:
-                    start_stats(b, k, HALVES)
+                    start_stats(b, k, 2 * HALVES)
+                if 0 == 0:
+                    nc.vector.memset(parts[(b, k)][:, :, 1 + HALVES + half : 2 + HALVES + half], 0.0)
                 square_scalar(b, k, half, slice(0, HALF_ROWS), 0, 1 + half)
             for bk in done:
                 stat_std(*bk)
             if u < N - UNITS_PER_BATCH:
                 square_scalar(b, k, half, slice(0, HALF_ROWS), 1, 1 + half)
+                if 0 > 0:
+                    for g in range(GROUPS_PER_PASS):
+                        square_vector(b, k, half, slice(0, 0), g, 1 + HALVES + half)
                 if half == 1:
                     complete.append((b, k))
             for b, half in now:
@@ -455,18 +468,12 @@ def tile_mlstmblock_pb_t_kernel(tc, h_attn, gn_w, gn_b, W_out, x, skip_scale, ou
                 quantise_w()
             if 1 <= u < N:
                 quantise(u - 1, 0, HALF_TOKENS)
-            if u == 1:
-                gram_trace(grams, 0, 1, 1)
-                stat_reduce(0, 1, HALVES)
-                stat_total(0, 1)
-                stat_square(0, 1)
-                stat_std(0, 1)
-                deviations.append((0, 1))
             if u + 1 < N:
                 transposes(u + 1)
             if u == 0:
-                gram(grams, 0, 1, 1, slice(0, HALF_ROWS), False, True)
                 channel_sums(0, 1, 1, slice(0, HALF_ROWS), 1, HALVES)
+                stat_reduce(0, 1, HALVES)
+                stat_total(0, 1)
             if u < N - UNITS_PER_BATCH:
                 b = u // UNITS_PER_BATCH + 1
                 k, half = divmod(u % UNITS_PER_BATCH, HALVES)

@@ -275,7 +275,7 @@ def tile_mlstmblock_pb_t_kernel(tc, h_attn, gn_w, gn_b, W_out, x, skip_scale, ou
         results = {}
 
         def on_vector(u):
-            return 2 if u < 12 or u == N - 1 else 0
+            return 2 if u < 13 or u == N - 1 else 0
 
         def bank_order(u):
             if on_vector(u) == 0:
@@ -387,18 +387,21 @@ def tile_mlstmblock_pb_t_kernel(tc, h_attn, gn_w, gn_b, W_out, x, skip_scale, ou
                 out=out_view[b, :, r0 + rows.start : r0 + rows.stop, :], in_=results[(b, half)][:, rows, :]
             )
 
-        start_stats(0, 0, CHUNKS + 1)
-        grams = [mm_psum.tile([P, ROWS_PER_BANK, D_MODEL], F32, name="acc") for g in range(GROUPS_PER_PASS)]
+        start_stats(0, 0, CHUNKS + (1 if 0 > 0 else 0))
+        if 0 > 0:
+            grams = [mm_psum.tile([P, ROWS_PER_BANK, D_MODEL], F32, name="acc") for g in range(GROUPS_PER_PASS)]
         for c in range(CHUNKS):
             half, r0 = divmod(c * CHUNK_ROWS, HALF_ROWS)
             r1 = r0 + CHUNK_ROWS
-            square_scalar(0, 0, half, slice(r0, r1 - 1), 0, 1 + c)
-            square_vector(0, 0, half, slice(r0, r1 - 1), 1, 1 + c)
-            gram(grams, 0, 0, half, slice(r1 - 1, r1), c == 0, c == CHUNKS - 1)
+            square_scalar(0, 0, half, slice(r0, r1 - 0), 0, 1 + c)
+            square_vector(0, 0, half, slice(r0, r1 - 0), 1, 1 + c)
+            if 0 > 0:
+                gram(grams, 0, 0, half, slice(r1 - 0, r1), c == 0, c == CHUNKS - 1)
             channel_sums(0, 0, half, slice(r0, r1), c, CHUNKS)
             if 1 <= c < CHUNKS - 1:
                 transposes(0, [c - 1])
-        gram_trace(grams, 0, 0, 1 + CHUNKS)
+        if 0 > 0:
+            gram_trace(grams, 0, 0, 1 + CHUNKS)
         stat_reduce(0, 0, CHUNKS)
         stat_total(0, 0)
         start_stats(0, 1, HALVES)
@@ -411,19 +414,35 @@ def tile_mlstmblock_pb_t_kernel(tc, h_attn, gn_w, gn_b, W_out, x, skip_scale, ou
         nc.vector.tensor_copy(out=skip_f[:], in_=skip_bf[:])
         channel_sums(0, 1, 0, slice(0, HALF_ROWS), 0, HALVES)
 
+        def regroup_gpsimd(u, t0, t1):
+            nc.gpsimd.tensor_scalar(
+                out=grouped[u][:, t0:t1, :].rearrange("p (c i) t -> p c t i", i=4),
+                in0=planes[u][:, :, t0:t1].rearrange("p t (c i) -> p c t i", i=4),
+                scalar1=1.0,
+                scalar2=0.0,
+                op0=ALU.mult,
+                op1=ALU.add,
+            )
+
         ready = []
         complete = []
         deviations = []
         for u in range(N):
             now, ready = ready, []
             done, complete = complete, []
+            if 256 > 0:
+                for bk in deviations:
+                    stat_affine(*bk)
             if 1 <= u < N:
-                regroup(nc.vector.tensor_copy, u - 1, 0, HALF_TOKENS)
+                regroup(nc.vector.tensor_copy, u - 1, 0, HALF_TOKENS - 256 + (4 if 256 > 0 else 0))
+                if True:
+                    regroup_gpsimd(u - 1, HALF_TOKENS - 256, HALF_TOKENS)
             for b, k in done:
                 stat_reduce(b, k, HALVES)
                 stat_total(b, k)
-            for bk in deviations:
-                stat_affine(*bk)
+            if 256 == 0:
+                for bk in deviations:
+                    stat_affine(*bk)
             deviations = list(done)
             for b, half in now:
                 add_skip(b, half, 0)

@@ -106,7 +106,7 @@ def tile_mlstmblock_pb_t_kernel(tc, h_attn, gn_w, gn_b, W_out, x, skip_scale, ou
         make_identity(nc, ident_f[:])
         warm = consts.tile([P, 1], F32, name="warm")
         nc.vector.memset(warm[:], 1.0)
-        nc.scalar.activation(out=warm[:], in_=warm[:], func=ACT.Sqrt)
+        nc.scalar.activation(out=warm[:], in_=warm[:], func=ACT.Abs_reciprocal_sqrt)
         neg_col = consts.tile([P, 2], BF16, name="neg_col")
         nc.vector.memset(neg_col[:], -1.0)
         mean_mat = consts.tile([P, GROUPS_PER_PASS, P], F32, name="mean_mat")
@@ -218,12 +218,11 @@ def tile_mlstmblock_pb_t_kernel(tc, h_attn, gn_w, gn_b, W_out, x, skip_scale, ou
 
         def stat_std(b, k):
             std = stat_pool.tile([P, 1], F32, name="std")
-            nc.scalar.activation(out=std[:], in_=var_tiles[(b, k)][:], func=ACT.Sqrt, scale=-1.0, bias=EPS)
+            nc.scalar.activation(out=std[:], in_=var_tiles[(b, k)][:], func=ACT.Abs_reciprocal_sqrt, scale=-1.0, bias=EPS)
             std_tiles[(b, k)] = std
 
         def stat_affine(b, k):
-            rstd = stat_pool.tile([P, 1], F32, name="rstd")
-            nc.vector.reciprocal(out=rstd[:], in_=std_tiles[(b, k)][:])
+            rstd = std_tiles[(b, k)]
             scale = stat_pool.tile([P, PACK], F32, name="scale")
             nc.vector.tensor_scalar(out=scale[:], in0=gnw[:, k, :], scalar1=rstd[:, 0:1], scalar2=None, op0=ALU.mult)
             bias = stat_pool.tile([P, PACK], F32, name="bias")
@@ -278,7 +277,7 @@ def tile_mlstmblock_pb_t_kernel(tc, h_attn, gn_w, gn_b, W_out, x, skip_scale, ou
             return 2 if u < 13 or u == N - 1 else 0
 
         def bank_order(u):
-            if on_vector(u) == 0:
+            if on_vector(u) == 0 or (u % 3 == 1):
                 return [(1, pair, th) for th in range(2) for pair in range(2)]
             return [(0, 0, 0), (1, 1, 0), (0, 1, 0), (1, 1, 1)]
 
@@ -310,13 +309,24 @@ def tile_mlstmblock_pb_t_kernel(tc, h_attn, gn_w, gn_b, W_out, x, skip_scale, ou
                     n = HALF_TOKENS // 2
                     for e in range(2):
                         t = 2 * j + e
-                        nc.scalar.activation(
-                            out=plane[:, t, th * n : (th + 1) * n],
-                            in_=tp[:].bitcast(BF16).rearrange("p (i e) -> p e i", e=2)[:, e, :],
-                            func=ACT.Identity,
-                            scale=scale[:, t : t + 1],
-                            bias=bias[:, t : t + 1],
-                        )
+                        values = tp[:].bitcast(BF16).rearrange("p (i e) -> p e i", e=2)[:, e, :]
+                        if on_vector(u) > 0 and (t, th) in ((0, 0), (0, 1), (1, 0), (1, 1)):
+                            nc.vector.tensor_scalar(
+                                out=plane[:, t, th * n : (th + 1) * n],
+                                in0=values,
+                                scalar1=scale[:, t : t + 1],
+                                scalar2=bias[:, t : t + 1],
+                                op0=ALU.mult,
+                                op1=ALU.add,
+                            )
+                        else:
+                            nc.scalar.activation(
+                                out=plane[:, t, th * n : (th + 1) * n],
+                                in_=values,
+                                func=ACT.Identity,
+                                scale=scale[:, t : t + 1],
+                                bias=bias[:, t : t + 1],
+                            )
                 else:
                     nc.vector.tensor_scalar(
                         out=plane[:, j, :],
@@ -387,31 +397,23 @@ def tile_mlstmblock_pb_t_kernel(tc, h_attn, gn_w, gn_b, W_out, x, skip_scale, ou
                 out=out_view[b, :, r0 + rows.start : r0 + rows.stop, :], in_=results[(b, half)][:, rows, :]
             )
 
-        start_stats(0, 0, CHUNKS + (1 if 0 > 0 else 0))
-        if 0 > 0:
-            grams = [mm_psum.tile([P, ROWS_PER_BANK, D_MODEL], F32, name="acc") for g in range(GROUPS_PER_PASS)]
+        start_stats(0, 0, CHUNKS)
         for c in range(CHUNKS):
             half, r0 = divmod(c * CHUNK_ROWS, HALF_ROWS)
             r1 = r0 + CHUNK_ROWS
-            square_scalar(0, 0, half, slice(r0, r1 - 0), 0, 1 + c)
-            square_vector(0, 0, half, slice(r0, r1 - 0), 1, 1 + c)
-            if 0 > 0:
-                gram(grams, 0, 0, half, slice(r1 - 0, r1), c == 0, c == CHUNKS - 1)
+            square_scalar(0, 0, half, slice(r0, r1), 0, 1 + c)
+            square_vector(0, 0, half, slice(r0, r1), 1, 1 + c)
             channel_sums(0, 0, half, slice(r0, r1), c, CHUNKS)
             if 1 <= c < CHUNKS - 1:
                 transposes(0, [c - 1])
-        if 0 > 0:
-            gram_trace(grams, 0, 0, 1 + CHUNKS)
         stat_reduce(0, 0, CHUNKS)
         stat_total(0, 0)
-        start_stats(0, 1, HALVES)
-        square_vector(0, 1, 0, slice(0, HALF_ROWS), 1, 1)
         stat_square(0, 0)
-        square_scalar(0, 1, 0, slice(0, HALF_ROWS), 0, 1)
         stat_std(0, 0)
         stat_affine(0, 0)
         transposes(0, [2, 3])
         nc.vector.tensor_copy(out=skip_f[:], in_=skip_bf[:])
+        start_stats(0, 1, HALVES)
         channel_sums(0, 1, 0, slice(0, HALF_ROWS), 0, HALVES)
 
         def regroup_gpsimd(u, t0, t1):
@@ -430,20 +432,27 @@ def tile_mlstmblock_pb_t_kernel(tc, h_attn, gn_w, gn_b, W_out, x, skip_scale, ou
         for u in range(N):
             now, ready = ready, []
             done, complete = complete, []
-            if 256 > 0:
+            ahead = u < N - UNITS_PER_BATCH
+            b1 = u // UNITS_PER_BATCH + 1
+            k1, half1 = divmod(u % UNITS_PER_BATCH, HALVES)
+            by_gram = (b1, k1) == (1, 0)
+            if 384 > 0:
                 for bk in deviations:
                     stat_affine(*bk)
-            if 1 <= u < N:
-                regroup(nc.vector.tensor_copy, u - 1, 0, HALF_TOKENS - 256 + (4 if 256 > 0 else 0))
+            if u >= 1:
+                regroup(nc.vector.tensor_copy, u - 1, 0, HALF_TOKENS - 384 + (4 if 384 > 0 else 0))
                 if True:
-                    regroup_gpsimd(u - 1, HALF_TOKENS - 256, HALF_TOKENS)
+                    regroup_gpsimd(u - 1, HALF_TOKENS - 384, HALF_TOKENS)
+            if 384 == 0:
+                for bk in deviations:
+                    stat_affine(*bk)
+            if u == 3:
+                done.append((1, 0))
+                gram_trace(grams, 1, 0, 1)
+            deviations = list(done)
             for b, k in done:
                 stat_reduce(b, k, HALVES)
                 stat_total(b, k)
-            if 256 == 0:
-                for bk in deviations:
-                    stat_affine(*bk)
-            deviations = list(done)
             for b, half in now:
                 add_skip(b, half, 0)
                 multiply(b, half, 2)
@@ -451,32 +460,30 @@ def tile_mlstmblock_pb_t_kernel(tc, h_attn, gn_w, gn_b, W_out, x, skip_scale, ou
                 multiply(b, half, 3)
             normalise(u)
             if u == 0:
-                for g in range(GROUPS_PER_PASS):
-                    square_vector(0, 1, 1, slice(0, HALF_ROWS), g, 2)
+                square_vector(0, 1, 0, slice(0, HALF_ROWS), 1, 1)
+                square_scalar(0, 1, 0, slice(0, HALF_ROWS), 0, 1)
             if u == 1:
+                square_scalar(0, 1, 1, slice(0, HALF_ROWS), 0, 2)
+                square_vector(0, 1, 1, slice(0, HALF_ROWS), 1, 2)
+                stat_reduce(0, 1, HALVES)
+                stat_total(0, 1)
                 stat_square(0, 1)
                 stat_std(0, 1)
                 deviations.append((0, 1))
                 transpose_w()
             for bk in done:
                 stat_square(*bk)
-            if u < N - UNITS_PER_BATCH:
-                b = u // UNITS_PER_BATCH + 1
-                k, half = divmod(u % UNITS_PER_BATCH, HALVES)
-                if half == 0:
-                    start_stats(b, k, 2 * HALVES)
-                if 0 == 0:
-                    nc.vector.memset(parts[(b, k)][:, :, 1 + HALVES + half : 2 + HALVES + half], 0.0)
-                square_scalar(b, k, half, slice(0, HALF_ROWS), 0, 1 + half)
+            if ahead:
+                if half1 == 0:
+                    start_stats(b1, k1, 1 if by_gram else HALVES)
+                if not by_gram:
+                    square_scalar(b1, k1, half1, slice(0, HALF_ROWS), 0, 1 + half1)
             for bk in done:
                 stat_std(*bk)
-            if u < N - UNITS_PER_BATCH:
-                square_scalar(b, k, half, slice(0, HALF_ROWS), 1, 1 + half)
-                if 0 > 0:
-                    for g in range(GROUPS_PER_PASS):
-                        square_vector(b, k, half, slice(0, 0), g, 1 + HALVES + half)
-                if half == 1:
-                    complete.append((b, k))
+            if ahead and not by_gram:
+                square_scalar(b1, k1, half1, slice(0, HALF_ROWS), 1, 1 + half1)
+                if half1 == 1:
+                    complete.append((b1, k1))
             for b, half in now:
                 add_skip(b, half, 2)
                 add_skip(b, half, 3)
@@ -485,38 +492,37 @@ def tile_mlstmblock_pb_t_kernel(tc, h_attn, gn_w, gn_b, W_out, x, skip_scale, ou
                     load_x(b + 2, half)
             if u == 2:
                 quantise_w()
-            if 1 <= u < N:
+            if u >= 1:
                 quantise(u - 1, 0, HALF_TOKENS)
             if u + 1 < N:
                 transposes(u + 1)
             if u == 0:
                 channel_sums(0, 1, 1, slice(0, HALF_ROWS), 1, HALVES)
-                stat_reduce(0, 1, HALVES)
-                stat_total(0, 1)
-            if u < N - UNITS_PER_BATCH:
-                b = u // UNITS_PER_BATCH + 1
-                k, half = divmod(u % UNITS_PER_BATCH, HALVES)
-                channel_sums(b, k, half, slice(0, HALF_ROWS), half, HALVES)
-            if 1 <= u < N:
-                b, k, half = units[u - 1]
-                if k == PASSES - 1:
-                    ready.append((b, half))
-                    multiply(b, half, 0)
-                    multiply(b, half, 1)
+            if ahead:
+                if by_gram:
+                    if half1 == 0:
+                        grams = [mm_psum.tile([P, ROWS_PER_BANK, D_MODEL], F32, name="acc") for g in range(GROUPS_PER_PASS)]
+                    gram(grams, b1, k1, half1, slice(0, HALF_ROWS), half1 == 0, half1 == 1)
+                channel_sums(b1, k1, half1, slice(0, HALF_ROWS), half1, HALVES)
+            if u >= 1:
+                bq, kq, hq = units[u - 1]
+                if kq == PASSES - 1:
+                    ready.append((bq, hq))
+                    multiply(bq, hq, 0)
+                    multiply(bq, hq, 1)
         u = N - 1
         b, k, half = units[u]
-        regroup(nc.scalar.copy, u, 512, 768)
-        regroup(nc.vector.tensor_copy, u, 0, 512)
-        regroup(nc.vector.tensor_copy, u, 768, 1024)
-        quantise(u, 0, 512)
-        multiply(b, half, 0)
-        multiply(b, half, 1)
-        quantise(u, 512, 1024)
-        multiply(b, half, 2)
-        multiply(b, half, 3)
-        add_skip(b, half, 0)
-        add_skip(b, half, 1)
-        store(b, half, slice(0, HALF_ROWS // 2))
+        for q in range(2):
+            t0 = q * 512
+            regroup(nc.scalar.copy, u, t0 + 256, t0 + 512)
+            regroup(nc.vector.tensor_copy, u, t0, t0 + 256)
+            quantise(u, t0, t0 + 512)
+            multiply(b, half, 2 * q)
+            multiply(b, half, 2 * q + 1)
+            if q == 1:
+                add_skip(b, half, 0)
+                add_skip(b, half, 1)
+                store(b, half, slice(0, HALF_ROWS // 2))
         add_skip(b, half, 2)
         add_skip(b, half, 3)
         store(b, half, slice(HALF_ROWS // 2, HALF_ROWS))

@@ -436,14 +436,14 @@ def tile_mlstmblock_pb_t_kernel(tc, h_attn, gn_w, gn_b, W_out, x, skip_scale, ou
             b1 = u // UNITS_PER_BATCH + 1
             k1, half1 = divmod(u % UNITS_PER_BATCH, HALVES)
             by_gram = (b1, k1) == (1, 0)
-            if 384 > 0:
+            if 320 > 0:
                 for bk in deviations:
                     stat_affine(*bk)
             if u >= 1:
-                regroup(nc.vector.tensor_copy, u - 1, 0, HALF_TOKENS - 384 + (4 if 384 > 0 else 0))
+                regroup(nc.vector.tensor_copy, u - 1, 0, HALF_TOKENS - 320 + (4 if 320 > 0 else 0))
                 if True:
-                    regroup_gpsimd(u - 1, HALF_TOKENS - 384, HALF_TOKENS)
-            if 384 == 0:
+                    regroup_gpsimd(u - 1, HALF_TOKENS - 320, HALF_TOKENS)
+            if 320 == 0:
                 for bk in deviations:
                     stat_affine(*bk)
             if u == 3:
@@ -495,7 +495,9 @@ def tile_mlstmblock_pb_t_kernel(tc, h_attn, gn_w, gn_b, W_out, x, skip_scale, ou
             if u >= 1:
                 quantise(u - 1, 0, HALF_TOKENS)
             if u + 1 < N:
-                transposes(u + 1)
+                transposes(u + 1, [0, 1])
+                if not (ahead and u > 3):
+                    transposes(u + 1, [2, 3])
             if u == 0:
                 channel_sums(0, 1, 1, slice(0, HALF_ROWS), 1, HALVES)
             if ahead:
@@ -504,6 +506,8 @@ def tile_mlstmblock_pb_t_kernel(tc, h_attn, gn_w, gn_b, W_out, x, skip_scale, ou
                         grams = [mm_psum.tile([P, ROWS_PER_BANK, D_MODEL], F32, name="acc") for g in range(GROUPS_PER_PASS)]
                     gram(grams, b1, k1, half1, slice(0, HALF_ROWS), half1 == 0, half1 == 1)
                 channel_sums(b1, k1, half1, slice(0, HALF_ROWS), half1, HALVES)
+            if ahead and u > 3:
+                transposes(u + 1, [2, 3])
             if u >= 1:
                 bq, kq, hq = units[u - 1]
                 if kq == PASSES - 1:
@@ -523,6 +527,6 @@ def tile_mlstmblock_pb_t_kernel(tc, h_attn, gn_w, gn_b, W_out, x, skip_scale, ou
                 add_skip(b, half, 0)
                 add_skip(b, half, 1)
                 store(b, half, slice(0, HALF_ROWS // 2))
-        add_skip(b, half, 2)
-        add_skip(b, half, 3)
-        store(b, half, slice(HALF_ROWS // 2, HALF_ROWS))
+        for pair in (2, 3):
+            add_skip(b, half, pair)
+            store(b, half, slice(ROWS_PER_BANK * pair, ROWS_PER_BANK * (pair + 1)))

from contextlib import ExitStack

import concourse.mybir as mybir
from concourse.masks import make_identity

FP8X4 = mybir.dt.float8_e4m3fn_x4
BF16 = mybir.dt.bfloat16
F32 = mybir.dt.float32
U32 = mybir.dt.uint32
U8 = mybir.dt.uint8
ALU = mybir.AluOpType
ACT = mybir.ActivationFunctionType
AXIS = mybir.AxisListType

P = 128
PACK = 4
K_PASS = P * PACK

BATCH, SEQ, CHANNELS, D_MODEL = 4, 2048, 1024, 256
GROUP = 256
EPS = 1e-5

PASSES = CHANNELS // K_PASS
GROUPS_PER_PASS = K_PASS // GROUP
GROUP_PARTS = GROUP // PACK
ROWS = SEQ // P
HALVES = 2
HALF_ROWS = ROWS // HALVES
HALF_TOKENS = HALF_ROWS * P
ROWS_PER_BANK = 2
PAIRS = HALF_ROWS // ROWS_PER_BANK
CHUNK_ROWS = 4
CHUNKS = ROWS // CHUNK_ROWS
UNITS_PER_BATCH = PASSES * HALVES

FLOPS = 2 * BATCH * SEQ * CHANNELS * D_MODEL


def tile_mlstmblock_pb_t_kernel(tc, h_attn, gn_w, gn_b, W_out, x, skip_scale, out):
    nc = tc.nc
    h_view = h_attn.rearrange("b (p r) c -> b p r c", r=ROWS)
    x_view = x.rearrange("b (p r) d -> b p r d", r=ROWS)
    out_view = out.rearrange("b (p r) d -> b p r d", r=ROWS)

    with ExitStack() as ctx:
        consts = ctx.enter_context(tc.tile_pool(name="consts", bufs=1))
        h_pool = ctx.enter_context(tc.tile_pool(name="h_pool", bufs=BATCH * UNITS_PER_BATCH))
        x_pool = ctx.enter_context(tc.tile_pool(name="x_pool", bufs=4))
        work = ctx.enter_context(tc.tile_pool(name="work", bufs=2))
        codes_pool = ctx.enter_context(tc.tile_pool(name="codes_pool", bufs=1))
        junk_pool = ctx.enter_context(tc.tile_pool(name="junk_pool", bufs=1))
        stat_pool = ctx.enter_context(tc.tile_pool(name="stat_pool", bufs=3))
        tp_psum = ctx.enter_context(tc.psum_pool(name="tp_psum", bufs=4))
        mm_psum = ctx.enter_context(tc.psum_pool(name="mm_psum", bufs=2))
        stat_psum = ctx.enter_context(tc.psum_pool(name="stat_psum", bufs=2))
        ctx.enter_context(tc.manual_schedule())

        h_tiles = {}
        x_tiles = {}

        def load_h(b, k, half, pieces=1):
            h_tile = h_pool.tile([P, HALF_ROWS, K_PASS], BF16, name="h_tile")
            n = HALF_ROWS // pieces
            for i in range(pieces):
                r0 = half * HALF_ROWS + i * n
                nc.sync.dma_start(
                    out=h_tile[:, i * n : (i + 1) * n, :],
                    in_=h_view[b, :, r0 : r0 + n, k * K_PASS : (k + 1) * K_PASS],
                )
            h_tiles[(b, k, half)] = h_tile

        def load_x(b, half):
            x_tile = x_pool.tile([P, HALF_ROWS, D_MODEL], BF16, name="x_tile")
            nc.sync.dma_start(out=x_tile[:], in_=x_view[b, :, half * HALF_ROWS : (half + 1) * HALF_ROWS, :])
            x_tiles[(b, half)] = x_tile

        gnw = consts.tile([P, PASSES, PACK], BF16, name="gnw")
        gnb = consts.tile([P, PASSES, PACK], BF16, name="gnb")
        nc.scalar.dma_start(out=gnw[:], in_=gn_w.rearrange("(k p t) -> p k t", p=P, t=PACK))
        nc.scalar.dma_start(out=gnb[:], in_=gn_b.rearrange("(k p t) -> p k t", p=P, t=PACK))
        skip_bf = consts.tile([P, 1], BF16, name="skip_bf")
        nc.scalar.dma_start(out=skip_bf[:], in_=skip_scale.partition_broadcast(P))

        load_h(0, 0, 0, 2)
        load_h(0, 0, 1, 2)
        load_h(0, 1, 0)
        load_h(0, 1, 1)
        w_raw = consts.tile([P, D_MODEL // P, CHANNELS], BF16, name="w_raw")
        nc.sync.dma_start(out=w_raw[:], in_=W_out.rearrange("(m p) c -> p m c", p=P))
        load_h(1, 0, 0)
        load_h(1, 0, 1)
        load_x(0, 0)
        load_x(0, 1)
        load_h(1, 1, 0)
        load_h(1, 1, 1)
        load_x(1, 0)
        load_x(1, 1)
        for b in (2, 3):
            for k in range(PASSES):
                for half in range(HALVES):
                    load_h(b, k, half)

        ident = consts.tile([P, P], BF16, name="ident")
        make_identity(nc, ident[:])
        ident_f = consts.tile([P, P], F32, name="ident_f")
        make_identity(nc, ident_f[:])
        warm = consts.tile([P, 1], F32, name="warm")
        nc.vector.memset(warm[:], 1.0)
        nc.scalar.activation(out=warm[:], in_=warm[:], func=ACT.Abs_reciprocal_sqrt)
        neg_col = consts.tile([P, 2], BF16, name="neg_col")
        nc.vector.memset(neg_col[:], -1.0)
        mean_mat = consts.tile([P, GROUPS_PER_PASS, P], F32, name="mean_mat")
        nc.vector.memset(mean_mat[:], 0.0)
        for g in range(GROUPS_PER_PASS):
            nc.vector.memset(mean_mat[:, g, g * GROUP_PARTS : (g + 1) * GROUP_PARTS], 1.0 / (SEQ * GROUP))
        skip_f = consts.tile([P, 1], F32, name="skip_f")

        parts = {}
        banks = {}
        n_cols = {}
        scale_bias = {}
        SUMS = 16

        def start_stats(b, k, n_squares):
            parts[(b, k)] = stat_pool.tile([P, GROUPS_PER_PASS, 8], F32, name="parts")
            banks[(b, k)] = stat_psum.tile([P, 32], F32, name="stat_bank")
            n_cols[(b, k)] = 1 + n_squares

        def square_scalar(b, k, half, rows, g, col):
            squares = junk_pool.tile([P, HALF_ROWS, GROUP], BF16, name="squares")
            n = rows.stop - rows.start
            nc.scalar.activation(
                out=squares[:, 0:n, :],
                in_=h_tiles[(b, k, half)][:, rows, g * GROUP : (g + 1) * GROUP],
                func=ACT.Square,
                accum_out=parts[(b, k)][:, g, col : col + 1],
            )

        def square_vector(b, k, half, rows, g, col):
            squares_v = junk_pool.tile([P, HALF_ROWS, GROUP], BF16, name="squares_v")
            n = rows.stop - rows.start
            x_in = h_tiles[(b, k, half)][:, rows, g * GROUP : (g + 1) * GROUP]
            nc.vector.scalar_tensor_tensor(
                out=squares_v[:, 0:n, :], in0=x_in, scalar=1.0, in1=x_in, op0=ALU.mult, op1=ALU.mult,
                accum_out=parts[(b, k)][:, g, col : col + 1],
            )

        def channel_sums(b, k, half, rows, seg, n_seg):
            for t in range(PACK):
                col = t * n_seg + seg
                for r in range(rows.start, rows.stop):
                    nc.tensor.matmul(
                        out=banks[(b, k)][:, col : col + 1],
                        lhsT=h_tiles[(b, k, half)][:, r, t * P : (t + 1) * P],
                        rhs=neg_col[:, 0:1],
                        start=(r == rows.start),
                        stop=(r == rows.stop - 1),
                    )

        def gram(grams, b, k, half, rows, first, last):
            for g in range(GROUPS_PER_PASS):
                for r in range(rows.start, rows.stop):
                    for j in range(GROUP // P):
                        block = h_tiles[(b, k, half)][:, r, g * GROUP + j * P : g * GROUP + (j + 1) * P]
                        nc.tensor.matmul(
                            out=grams[g][:, 0, 0:P],
                            lhsT=block,
                            rhs=block,
                            start=(first and r == rows.start and j == 0),
                            stop=(last and r == rows.stop - 1 and j == GROUP // P - 1),
                        )

        def gram_trace(grams, b, k, col):
            for g in range(GROUPS_PER_PASS):
                diag = junk_pool.tile([P, P], F32, name="diag")
                nc.vector.scalar_tensor_tensor(
                    out=diag[:], in0=grams[g][:, 0, 0:P], scalar=1.0, in1=ident_f[:], op0=ALU.mult, op1=ALU.mult,
                    accum_out=parts[(b, k)][:, g, col : col + 1],
                )

        def stat_reduce(b, k, n_seg):
            nc.vector.tensor_reduce(
                out=parts[(b, k)][:, :, 0:1].rearrange("p g o -> p (g o)"),
                in_=banks[(b, k)][:, 0 : PACK * n_seg].rearrange("p (g s) -> p g s", g=GROUPS_PER_PASS),
                axis=AXIS.X,
                op=ALU.add,
            )

        def stat_total(b, k):
            n = n_cols[(b, k)]
            for g in range(GROUPS_PER_PASS):
                nc.tensor.matmul(
                    out=banks[(b, k)][:, SUMS : SUMS + n],
                    lhsT=mean_mat[:, g, :],
                    rhs=parts[(b, k)][:, g, 0:n],
                    start=(g == 0),
                    stop=(g == GROUPS_PER_PASS - 1),
                )

        std_tiles = {}
        var_tiles = {}

        def stat_square(b, k):
            bank = banks[(b, k)]
            n = n_cols[(b, k)]
            ex2 = stat_pool.tile([P, 1], F32, name="ex2")
            nc.vector.tensor_reduce(out=ex2[:], in_=bank[:, SUMS + 1 : SUMS + n], axis=AXIS.X, op=ALU.add)
            neg_var = stat_pool.tile([P, 1], F32, name="neg_var")
            nc.vector.scalar_tensor_tensor(
                out=neg_var[:],
                in0=bank[:, SUMS : SUMS + 1],
                scalar=bank[:, SUMS : SUMS + 1],
                in1=ex2[:],
                op0=ALU.mult,
                op1=ALU.subtract,
            )
            var_tiles[(b, k)] = neg_var

        def stat_std(b, k):
            std = stat_pool.tile([P, 1], F32, name="std")
            nc.scalar.activation(out=std[:], in_=var_tiles[(b, k)][:], func=ACT.Abs_reciprocal_sqrt, scale=-1.0, bias=EPS)
            std_tiles[(b, k)] = std

        def stat_affine(b, k):
            rstd = std_tiles[(b, k)]
            scale = stat_pool.tile([P, PACK], F32, name="scale")
            nc.vector.tensor_scalar(out=scale[:], in0=gnw[:, k, :], scalar1=rstd[:, 0:1], scalar2=None, op0=ALU.mult)
            bias = stat_pool.tile([P, PACK], F32, name="bias")
            nc.vector.scalar_tensor_tensor(
                out=bias[:],
                in0=scale[:],
                scalar=banks[(b, k)][:, SUMS : SUMS + 1],
                in1=gnb[:, k, :],
                op0=ALU.mult,
                op1=ALU.add,
            )
            scale_bias[(b, k)] = (scale, bias)

        w_grouped = consts.tile([P, PASSES, D_MODEL, PACK], BF16, name="w_grouped", align_bytes=64)
        w_codes = consts.tile([P, PASSES * D_MODEL], U32, name="w_codes", align_bytes=64)
        w_scales = consts.tile([P, PASSES * D_MODEL], U8, name="w_scales", align_bytes=64)

        def transpose_w():
            for k in range(PASSES):
                w_ps = tp_psum.tile([P, 2, D_MODEL], F32, name="tp")
                for u in range(2):
                    for m in range(D_MODEL // P):
                        words = w_raw[:, m, :].bitcast(F32)
                        nc.tensor.transpose(
                            w_ps[:, u, m * P : (m + 1) * P],
                            words[:, k * 2 * P + u : (k + 1) * 2 * P : 2],
                            ident_f[:],
                        )
                nc.scalar.copy(
                    out=w_grouped[:, k].rearrange("p n t -> p (n t)").bitcast(F32).rearrange("p (n u) -> p n u", u=2),
                    in_=w_ps[:].rearrange("p u n -> p n u"),
                )

        def quantise_w():
            nc.vector.quantize_mx(
                out=w_codes[:].bitcast(FP8X4),
                scales=w_scales[:],
                in_=w_grouped[:].rearrange("p k n t -> p (k n t)"),
            )

        units = [(0, k, half) for k in range(PASSES) for half in range(HALVES)]
        units += [(b, k, half) for b in range(1, BATCH) for half in range(HALVES) for k in range(PASSES)]
        N = len(units)
        tps = {}
        planes = {}
        grouped = {}
        h_codes = {}
        accs = {}
        results = {}

        def on_vector(u):
            return 2 if u < 13 or u == N - 1 else 0

        def bank_order(u):
            if on_vector(u) == 0 or (u % 3 == 1):
                return [(1, pair, th) for th in range(2) for pair in range(2)]
            return [(0, 0, 0), (1, 1, 0), (0, 1, 0), (1, 1, 1)]

        def transposes(u, which=range(4)):
            b, k, half = units[u]
            h_tile = h_tiles[(b, k, half)]
            for key in [bank_order(u)[i] for i in which]:
                as_words, j, th = key
                if as_words:
                    tp = tp_psum.tile([P, HALF_TOKENS // 2], F32, name="tp")
                    for r in range(HALF_ROWS // 2):
                        words = h_tile[:, th * HALF_ROWS // 2 + r, :].bitcast(F32)
                        nc.tensor.transpose(tp[:, r * P : (r + 1) * P], words[:, j::2], ident_f[:])
                else:
                    tp = tp_psum.tile([P, HALF_TOKENS], BF16, name="tp")
                    for r in range(HALF_ROWS):
                        nc.tensor.transpose(tp[:, r * P : (r + 1) * P], h_tile[:, r, j::PACK], ident[:])
                tps[(u, key)] = tp

        def normalise(u):
            b, k, half = units[u]
            scale, bias = scale_bias[(b, k)]
            plane = work.tile([P, PACK, HALF_TOKENS], BF16, name="plane")
            planes[u] = plane
            for key in bank_order(u):
                as_words, j, th = key
                tp = tps[(u, key)]
                if as_words:
                    n = HALF_TOKENS // 2
                    for e in range(2):
                        t = 2 * j + e
                        values = tp[:].bitcast(BF16).rearrange("p (i e) -> p e i", e=2)[:, e, :]
                        if on_vector(u) > 0 and (t, th) in ((0, 0), (0, 1), (1, 0), (1, 1)):
                            nc.vector.tensor_scalar(
                                out=plane[:, t, th * n : (th + 1) * n],
                                in0=values,
                                scalar1=scale[:, t : t + 1],
                                scalar2=bias[:, t : t + 1],
                                op0=ALU.mult,
                                op1=ALU.add,
                            )
                        else:
                            nc.scalar.activation(
                                out=plane[:, t, th * n : (th + 1) * n],
                                in_=values,
                                func=ACT.Identity,
                                scale=scale[:, t : t + 1],
                                bias=bias[:, t : t + 1],
                            )
                else:
                    nc.vector.tensor_scalar(
                        out=plane[:, j, :],
                        in0=tp[:],
                        scalar1=scale[:, j : j + 1],
                        scalar2=bias[:, j : j + 1],
                        op0=ALU.mult,
                        op1=ALU.add,
                    )

        def regroup(copy, u, t0, t1):
            if u not in grouped:
                grouped[u] = work.tile([P, HALF_TOKENS, PACK], BF16, name="grp", align_bytes=64)
            copy(
                out=grouped[u][:, t0:t1, :].rearrange("p (c i) t -> p c t i", i=4),
                in_=planes[u][:, :, t0:t1].rearrange("p t (c i) -> p c t i", i=4),
            )

        def quantise(u, t0, t1):
            b, k, half = units[u]
            if t0 == 0:
                codes = codes_pool.tile([P, HALF_TOKENS], U32, name="codes%d%d" % (k, half), align_bytes=64)
                scales = codes_pool.tile([P, HALF_TOKENS], U8, name="scales%d%d" % (k, half), align_bytes=64)
                h_codes[(k, half)] = (codes, scales)
            codes, scales = h_codes[(k, half)]
            nc.vector.quantize_mx(
                out=codes[:, t0:t1].bitcast(FP8X4),
                scales=scales[:, t0:t1],
                in_=grouped[u][:, t0:t1, :].rearrange("p r t -> p (r t)"),
            )

        def multiply(b, half, pair):
            if (b, half) == (BATCH - 1, HALVES - 1) and pair >= 2:
                acc = tp_psum.tile([P, ROWS_PER_BANK, D_MODEL], F32, name="tp")
            else:
                acc = mm_psum.tile([P, ROWS_PER_BANK, D_MODEL], F32, name="acc")
            for s in range(ROWS_PER_BANK):
                r = ROWS_PER_BANK * pair + s
                for k in range(PASSES):
                    codes, scales = h_codes[(k, half)]
                    nc.tensor.matmul_mx(
                        out=acc[:, s, :],
                        lhsT=codes[:, r * P : (r + 1) * P].bitcast(FP8X4),
                        lhsT_scale=scales[:, r * P : (r + 1) * P],
                        rhs=w_codes[:, k * D_MODEL : (k + 1) * D_MODEL].bitcast(FP8X4),
                        rhs_scale=w_scales[:, k * D_MODEL : (k + 1) * D_MODEL],
                        start=(k == 0),
                        stop=(k == PASSES - 1),
                    )
            accs[(b, half, pair)] = acc

        def add_skip(b, half, pair):
            if pair == 0:
                results[(b, half)] = work.tile([P, HALF_ROWS, D_MODEL], F32, name="result")
            rows = slice(ROWS_PER_BANK * pair, ROWS_PER_BANK * (pair + 1))
            nc.vector.scalar_tensor_tensor(
                out=results[(b, half)][:, rows, :].rearrange("p s d -> p (s d)"),
                in0=x_tiles[(b, half)][:, rows, :].rearrange("p s d -> p (s d)"),
                scalar=skip_f[:, 0:1],
                in1=accs[(b, half, pair)][:].rearrange("p s d -> p (s d)"),
                op0=ALU.mult,
                op1=ALU.add,
            )

        def store(b, half, rows):
            r0 = half * HALF_ROWS
            nc.sync.dma_start(
                out=out_view[b, :, r0 + rows.start : r0 + rows.stop, :], in_=results[(b, half)][:, rows, :]
            )

        start_stats(0, 0, CHUNKS)
        for c in range(CHUNKS):
            half, r0 = divmod(c * CHUNK_ROWS, HALF_ROWS)
            r1 = r0 + CHUNK_ROWS
            square_scalar(0, 0, half, slice(r0, r1), 0, 1 + c)
            square_vector(0, 0, half, slice(r0, r1), 1, 1 + c)
            channel_sums(0, 0, half, slice(r0, r1), c, CHUNKS)
            if 1 <= c < CHUNKS - 1:
                transposes(0, [c - 1])
        stat_reduce(0, 0, CHUNKS)
        stat_total(0, 0)
        stat_square(0, 0)
        stat_std(0, 0)
        stat_affine(0, 0)
        transposes(0, [2, 3])
        nc.vector.tensor_copy(out=skip_f[:], in_=skip_bf[:])
        start_stats(0, 1, HALVES)
        channel_sums(0, 1, 0, slice(0, HALF_ROWS), 0, HALVES)

        def regroup_gpsimd(u, t0, t1):
            nc.gpsimd.tensor_scalar(
                out=grouped[u][:, t0:t1, :].rearrange("p (c i) t -> p c t i", i=4),
                in0=planes[u][:, :, t0:t1].rearrange("p t (c i) -> p c t i", i=4),
                scalar1=1.0,
                scalar2=0.0,
                op0=ALU.mult,
                op1=ALU.add,
            )

        ready = []
        complete = []
        deviations = []
        for u in range(N):
            now, ready = ready, []
            done, complete = complete, []
            ahead = u < N - UNITS_PER_BATCH
            b1 = u // UNITS_PER_BATCH + 1
            k1, half1 = divmod(u % UNITS_PER_BATCH, HALVES)
            by_gram = (b1, k1) == (1, 0)
            if 320 > 0:
                for bk in deviations:
                    stat_affine(*bk)
            if u >= 1:
                regroup(nc.vector.tensor_copy, u - 1, 0, HALF_TOKENS - 320 + (4 if 320 > 0 else 0))
                if True:
                    regroup_gpsimd(u - 1, HALF_TOKENS - 320, HALF_TOKENS)
            if 320 == 0:
                for bk in deviations:
                    stat_affine(*bk)
            if u == 3:
                done.append((1, 0))
                gram_trace(grams, 1, 0, 1)
            deviations = list(done)
            for b, k in done:
                stat_reduce(b, k, HALVES)
                stat_total(b, k)
            for b, half in now:
                add_skip(b, half, 0)
                multiply(b, half, 2)
                add_skip(b, half, 1)
                multiply(b, half, 3)
            normalise(u)
            if u == 0:
                square_vector(0, 1, 0, slice(0, HALF_ROWS), 1, 1)
                square_scalar(0, 1, 0, slice(0, HALF_ROWS), 0, 1)
            if u == 1:
                square_scalar(0, 1, 1, slice(0, HALF_ROWS), 0, 2)
                square_vector(0, 1, 1, slice(0, HALF_ROWS), 1, 2)
                stat_reduce(0, 1, HALVES)
                stat_total(0, 1)
                stat_square(0, 1)
                stat_std(0, 1)
                deviations.append((0, 1))
                transpose_w()
            for bk in done:
                stat_square(*bk)
            if ahead:
                if half1 == 0:
                    start_stats(b1, k1, 1 if by_gram else HALVES)
                if not by_gram:
                    square_scalar(b1, k1, half1, slice(0, HALF_ROWS), 0, 1 + half1)
            for bk in done:
                stat_std(*bk)
            if ahead and not by_gram:
                square_scalar(b1, k1, half1, slice(0, HALF_ROWS), 1, 1 + half1)
                if half1 == 1:
                    complete.append((b1, k1))
            for b, half in now:
                add_skip(b, half, 2)
                add_skip(b, half, 3)
                store(b, half, slice(0, HALF_ROWS))
                if 2 * b + half + 4 < 2 * BATCH:
                    load_x(b + 2, half)
            if u == 2:
                quantise_w()
            if u >= 1:
                quantise(u - 1, 0, HALF_TOKENS)
            if u + 1 < N:
                transposes(u + 1, [0, 1])
                if not (ahead and u > 3):
                    transposes(u + 1, [2, 3])
            if u == 0:
                channel_sums(0, 1, 1, slice(0, HALF_ROWS), 1, HALVES)
            if ahead:
                if by_gram:
                    if half1 == 0:
                        grams = [mm_psum.tile([P, ROWS_PER_BANK, D_MODEL], F32, name="acc") for g in range(GROUPS_PER_PASS)]
                    gram(grams, b1, k1, half1, slice(0, HALF_ROWS), half1 == 0, half1 == 1)
                channel_sums(b1, k1, half1, slice(0, HALF_ROWS), half1, HALVES)
            if ahead and u > 3:
                transposes(u + 1, [2, 3])
            if u >= 1:
                bq, kq, hq = units[u - 1]
                if kq == PASSES - 1:
                    ready.append((bq, hq))
                    multiply(bq, hq, 0)
                    multiply(bq, hq, 1)
        u = N - 1
        b, k, half = units[u]
        for q in range(2):
            t0 = q * 512
            regroup(nc.scalar.copy, u, t0 + 256, t0 + 512)
            regroup(nc.vector.tensor_copy, u, t0, t0 + 256)
            quantise(u, t0, t0 + 512)
            multiply(b, half, 2 * q)
            multiply(b, half, 2 * q + 1)
            if q == 1:
                add_skip(b, half, 0)
                add_skip(b, half, 1)
                store(b, half, slice(0, HALF_ROWS // 2))
        for pair in (2, 3):
            add_skip(b, half, pair)
            store(b, half, slice(ROWS_PER_BANK * pair, ROWS_PER_BANK * (pair + 1)))
